import numpy as np
import ml_dtypes


def mxq(x, axis, fmt="e4m3"):
    dtype, down = {"e4m3": (ml_dtypes.float8_e4m3fn, 7), "e5m2": (ml_dtypes.float8_e5m2, 14)}[fmt]
    v = np.moveaxis(np.asarray(x, np.float32).astype(ml_dtypes.bfloat16).astype(np.float64), axis, -1)
    blocks = v.reshape(v.shape[:-1] + (-1, 32))
    amax = np.abs(blocks).max(-1, keepdims=True)
    byte = np.maximum(np.where(amax > 0, np.frexp(amax)[1] - 1 + 127, 0) - down, 1)
    scale = np.exp2(byte - 127.0)
    codes = (blocks / scale).astype(np.float32).astype(dtype).astype(np.float64)
    return np.moveaxis((codes * scale).reshape(v.shape), -1, axis)


WIDE = False


def mx_kscale(k):
    if not WIDE:
        return np.ones(k)
    levels = np.array([10, -10, 5, -5, 0])
    a = np.random.permutation(np.resize(levels, k // 512 * 4)).reshape(k // 512, 4)
    idx = np.arange(k)
    return np.exp2(a[idx // 512, idx % 128 // 32])


BF16 = ml_dtypes.bfloat16


def bf(x):
    return np.asarray(x, np.float32).astype(BF16)


def f64(x):
    return np.asarray(x).astype(np.float64)


B, D, C = 512, 256, 128
EPS_SQRT = 1e-10
EPS_NORM = 1e-12


def setup_inputs():
    s = mx_kscale(D * D)
    a = np.round(np.log2(np.array([s.max(), s.min()])) / 2)
    r = np.repeat(np.exp2(a - a.min()), D // 2)
    g = np.exp2(np.round(np.log2(np.mean(r ** 2))))
    return {"feat": bf(np.random.standard_normal((B, D)) * r ** 2),
            "W": bf(np.random.standard_normal((C, D * D)) * g / np.outer(r, r).reshape(-1)),
            "b": bf(np.random.standard_normal(C) * 0.3)}


def reference(feat, W, b):
    feat = f64(feat)
    x = (feat[:, :, None] * feat[:, None, :]).reshape(feat.shape[0], -1)
    x = np.sign(x) * np.sqrt(np.abs(x) + EPS_SQRT)
    norm = np.maximum(np.linalg.norm(x, axis=1, keepdims=True), EPS_NORM)
    x = x / norm
    return (mxq(x, 1, "e4m3") @ mxq(f64(W), 1, "e4m3").T) + f64(b)

@@ -1,0 +1,233 @@
+from contextlib import ExitStack
+
+import concourse.mybir as mybir
+from concourse.masks import make_identity
+
+FP8X4 = mybir.dt.float8_e4m3fn_x4
+BF16 = mybir.dt.bfloat16
+F32 = mybir.dt.float32
+U32 = mybir.dt.uint32
+U8 = mybir.dt.uint8
+ACT = mybir.ActivationFunctionType
+ALU = mybir.AluOpType
+AX = mybir.AxisListType
+
+B, D, C = 512, 256, 128
+P = 128
+PACK = 4
+NL = P // PACK
+NG = B // NL
+NM = D // PACK
+EPS_SQRT = 1e-10
+EPS_NORM = 1e-12
+MM = 8
+FLOPS = 2 * B * D * D * C
+
+
+def tile_bcnnresnet_kernel(tc, feat, W, b, out):
+    nc = tc.nc
+    with ExitStack() as ctx:
+        const = ctx.enter_context(tc.tile_pool(name="const", bufs=1))
+        zpool = ctx.enter_context(tc.tile_pool(name="zpool", bufs=3))
+        xpool = ctx.enter_context(tc.tile_pool(name="xpool", bufs=3))
+        gpool = ctx.enter_context(tc.tile_pool(name="gpool", bufs=4))
+        cpool = ctx.enter_context(tc.tile_pool(name="cpool", bufs=4))
+        wpool = ctx.enter_context(tc.tile_pool(name="wpool", bufs=3))
+        gwpool = ctx.enter_context(tc.tile_pool(name="gwpool", bufs=3))
+        accp = ctx.enter_context(tc.psum_pool(name="accp", bufs=1))
+        tps = ctx.enter_context(tc.psum_pool(name="tps", bufs=5))
+        wps = ctx.enter_context(tc.psum_pool(name="wps", bufs=2))
+
+        F = const.tile([P, NG, D], BF16, name="F")
+        feat_v = feat.rearrange("(g nl) j -> nl g j", nl=NL)
+        queues = [nc.sync, nc.scalar, nc.gpsimd, nc.sync]
+        for t in range(PACK):
+            queues[t].dma_start(out=F[t:P:PACK, :, :], in_=feat_v)
+        bb = const.tile([P, C], BF16, name="bb")
+        nc.gpsimd.dma_start(out=bb[:], in_=b.partition_broadcast(P))
+
+        W_v = W.rearrange("(gc cl) (m t j) -> t gc cl m j", cl=NL, t=PACK, j=D)
+        w_tiles = {}
+
+        def load_w(ch):
+            Wp = wpool.tile([P, PACK, MM, D], BF16, name="Wp")
+            for gc in range(PACK):
+                for t in range(PACK):
+                    nc.sync.dma_start(out=Wp[t:P:PACK, gc, :, :], in_=W_v[t, gc, :, ch * MM:(ch + 1) * MM, :])
+            w_tiles[ch] = Wp
+
+        load_w(0)
+        load_w(1)
+
+        ident_bf = const.tile([P, P], BF16, name="ident_bf")
+        make_identity(nc, ident_bf[:])
+        ident_f = const.tile([P, P], F32, name="ident_f")
+        make_identity(nc, ident_f[:])
+
+        M4f = const.tile([P, PACK], F32, name="M4f")
+        nc.vector.tensor_reduce(out=M4f[:], in_=ident_bf[:].rearrange("q (nl t) -> q t nl", t=PACK), axis=AX.X, op=ALU.add)
+        M4 = const.tile([P, PACK], BF16, name="M4")
+        nc.vector.tensor_copy(out=M4[:], in_=M4f[:])
+
+        A = const.tile([P, NG, D], BF16, name="A")
+        junk = const.tile([P, D], BF16, name="junk")
+        Ssum = const.tile([P, NG], F32, name="Ssum")
+        nz = const.tile([P, NG], F32, name="nz")
+        for g in range(NG):
+            nc.scalar.activation(out=A[:, g, :], in_=F[:, g, :], func=ACT.Abs, accum_out=Ssum[:, g:g + 1])
+        for g in range(NG):
+            nc.scalar.activation(out=junk[:], in_=A[:, g, :], func=ACT.Sign, accum_out=nz[:, g:g + 1])
+
+        prod = const.tile([P, NG * NM, PACK], BF16, name="prod")
+        nc.vector.tensor_tensor(
+            out=prod[:],
+            in0=F[:].rearrange("q g (m t) -> q (g m) t", t=PACK),
+            in1=M4[:].unsqueeze(1).to_broadcast([P, NG * NM, PACK]),
+            op=ALU.mult,
+        )
+        FI = const.tile([P, NG * NM], F32, name="FI")
+        nc.vector.tensor_reduce(out=FI[:], in_=prod[:], axis=AX.X, op=ALU.add)
+        SI = const.tile([P, NG * NM], F32, name="SI")
+        nc.scalar.activation(out=SI[:], in_=FI[:], func=ACT.Sign)
+
+        SJT = []
+        for J in range(2):
+            sj = const.tile([P, NG * P], BF16, name="SJT%d" % J)
+            for h in range(2):
+                ps = tps.tile([P, 8 * P], BF16, name="ps", tag="t")
+                for gg in range(8):
+                    nc.tensor.transpose(out=ps[:, gg * P:(gg + 1) * P], in_=F[:, 8 * h + gg, J * P:(J + 1) * P], identity=ident_bf[:])
+                nc.scalar.activation(out=sj[:, h * 1024:(h + 1) * 1024], in_=ps[:], func=ACT.Sign)
+            SJT.append(sj)
+
+        def small(name):
+            return const.tile([P, NG], F32, name=name)
+
+        sq, nq, nqe, n2, nrm, nrc, rn0, r2, hh, hn, rn, rn2, beta = [
+            small(n) for n in ("sq", "nq", "nqe", "n2", "nrm", "nrc", "rn0", "r2", "hh", "hn", "rn", "rn2", "beta")
+        ]
+        nc.vector.tensor_tensor(out=sq[:], in0=Ssum[:], in1=Ssum[:], op=ALU.mult)
+        nc.vector.tensor_tensor(out=nq[:], in0=nz[:], in1=nz[:], op=ALU.mult)
+        nc.vector.tensor_scalar(out=nqe[:], in0=nq[:], scalar1=EPS_SQRT, scalar2=None, op0=ALU.mult)
+        nc.vector.tensor_tensor(out=n2[:], in0=sq[:], in1=nqe[:], op=ALU.add)
+        nc.scalar.activation(out=nrm[:], in_=n2[:], func=ACT.Sqrt)
+        nc.vector.tensor_scalar(out=nrc[:], in0=nrm[:], scalar1=EPS_NORM, scalar2=None, op0=ALU.max)
+        nc.vector.reciprocal(out=rn0[:], in_=nrc[:])
+        nc.vector.tensor_tensor(out=r2[:], in0=rn0[:], in1=rn0[:], op=ALU.mult)
+        nc.vector.tensor_tensor(out=hh[:], in0=r2[:], in1=n2[:], op=ALU.mult)
+        nc.vector.tensor_scalar(out=hn[:], in0=hh[:], scalar1=-0.5, scalar2=1.5, op0=ALU.mult, op1=ALU.add)
+        nc.vector.tensor_tensor(out=rn[:], in0=rn0[:], in1=hn[:], op=ALU.mult)
+        nc.vector.tensor_tensor(out=rn2[:], in0=rn[:], in1=rn[:], op=ALU.mult)
+        nc.vector.tensor_scalar(out=beta[:], in0=rn2[:], scalar1=EPS_SQRT, scalar2=None, op0=ALU.mult)
+
+        AI = const.tile([P, NG * NM], F32, name="AI")
+        nc.vector.tensor_tensor(out=AI[:], in0=FI[:], in1=SI[:], op=ALU.mult)
+        alpha = const.tile([P, NG * NM], F32, name="alpha")
+        nc.vector.tensor_tensor(
+            out=alpha[:].rearrange("q (g m) -> q g m", m=NM),
+            in0=AI[:].rearrange("q (g m) -> q g m", m=NM),
+            in1=rn2[:].unsqueeze(2).to_broadcast([P, NG, NM]),
+            op=ALU.mult,
+        )
+
+        acc = accp.tile([P, B], F32, name="acc")
+
+        z_tiles, x_tiles, t_tiles, wq_tiles, xq_tiles = {}, {}, {}, {}, {}
+
+        def stage_sqrt(m):
+            Z = zpool.tile([P, NG, D], BF16, name="Z")
+            for g in range(NG):
+                col = g * NM + m
+                nc.scalar.activation(out=Z[:, g, :], in_=A[:, g, :], func=ACT.Sqrt, bias=beta[:, g:g + 1], scale=alpha[:, col:col + 1])
+            z_tiles[m] = Z
+
+        def stage_sign_i(m):
+            Z = z_tiles.pop(m)
+            X = xpool.tile([P, NG, D], BF16, name="X")
+            for g in range(NG):
+                col = g * NM + m
+                nc.vector.tensor_scalar(out=X[:, g, :], in0=Z[:, g, :], scalar1=SI[:, col:col + 1], scalar2=None, op0=ALU.mult)
+            x_tiles[m] = X
+
+        def stage_w(m):
+            Wp = w_tiles[m // MM]
+            ps = wps.tile([P, 8 * P], BF16, name="wt")
+            for J in range(2):
+                for gc in range(PACK):
+                    o = (J * PACK + gc) * P
+                    nc.tensor.transpose(out=ps[:, o:o + P], in_=Wp[:, gc, m % MM, J * P:(J + 1) * P], identity=ident_bf[:])
+            Gw = gwpool.tile([P, 8 * P], BF16, name="Gw", align_bytes=64)
+            nc.scalar.copy(out=Gw[:], in_=ps[:])
+            Wc = gwpool.tile([P, 2 * P], U32, name="Wc", align_bytes=64)
+            Ws = gwpool.tile([P, 2 * P], U8, name="Ws", align_bytes=64)
+            nc.vector.quantize_mx(out=Wc[:].bitcast(FP8X4), scales=Ws[:], in_=Gw[:])
+            wq_tiles[m] = (Wc, Ws)
+
+        def stage_t(m, J):
+            X = x_tiles[m]
+            pss = []
+            for h in range(2):
+                ps = tps.tile([P, 8 * P], BF16, name="ps", tag="t")
+                for gg in range(8):
+                    nc.tensor.transpose(out=ps[:, gg * P:(gg + 1) * P], in_=X[:, 8 * h + gg, J * P:(J + 1) * P], identity=ident_bf[:])
+                pss.append(ps)
+            t_tiles[(m, J)] = pss
+
+        def stage_q(m, J):
+            pss = t_tiles.pop((m, J))
+            G = gpool.tile([P, NG * P], BF16, name="G", align_bytes=64)
+            for h in range(2):
+                nc.vector.tensor_tensor(out=G[:, h * 1024:(h + 1) * 1024], in0=pss[h][:], in1=SJT[J][:, h * 1024:(h + 1) * 1024], op=ALU.mult)
+            Xc = cpool.tile([P, B], U32, name="Xc", align_bytes=64)
+            Xs = cpool.tile([P, B], U8, name="Xs", align_bytes=64)
+            nc.vector.quantize_mx(out=Xc[:].bitcast(FP8X4), scales=Xs[:], in_=G[:])
+            xq_tiles[(m, J)] = (Xc, Xs)
+
+        def stage_mx(m, J):
+            Wc, Ws = wq_tiles[m]
+            Xc, Xs = xq_tiles.pop((m, J))
+            nc.tensor.matmul_mx(
+                out=acc[:],
+                lhsT=Wc[:, J * P:(J + 1) * P].bitcast(FP8X4),
+                lhsT_scale=Ws[:, J * P:(J + 1) * P],
+                rhs=Xc[:].bitcast(FP8X4),
+                rhs_scale=Xs[:],
+                start=(m == 0 and J == 0),
+                stop=(m == NM - 1 and J == 1),
+            )
+
+        stage_sqrt(0)
+        stage_sqrt(1)
+        stage_sign_i(0)
+        stage_w(0)
+        for m in range(NM):
+            if m % MM == 0 and m // MM + 2 < NM // MM:
+                load_w(m // MM + 2)
+            if m + 2 < NM:
+                stage_sqrt(m + 2)
+            if m + 1 < NM:
+                stage_sign_i(m + 1)
+                stage_w(m + 1)
+            stage_t(m, 0)
+            stage_t(m, 1)
+            if m > 0:
+                stage_mx(m - 1, 0)
+                stage_mx(m - 1, 1)
+            stage_q(m, 0)
+            stage_q(m, 1)
+        stage_mx(NM - 1, 0)
+        stage_mx(NM - 1, 1)
+
+        accS = const.tile([P, B], F32, name="accS")
+        nc.vector.tensor_copy(out=accS[:], in_=acc[:])
+        pso = tps.tile([P, B], F32, name="pso", tag="t")
+        for nb in range(B // P):
+            nc.tensor.transpose(out=pso[:, nb * P:(nb + 1) * P], in_=accS[:, nb * P:(nb + 1) * P], identity=ident_f[:])
+        res = const.tile([P, B // P, C], F32, name="res")
+        nc.vector.tensor_tensor(
+            out=res[:],
+            in0=pso[:].rearrange("p (nb c) -> p nb c", c=C),
+            in1=bb[:].unsqueeze(1).to_broadcast([P, B // P, C]),
+            op=ALU.add,
+        )
+        nc.sync.dma_start(out=out.rearrange("(nb p) c -> p nb c", p=P), in_=res[:])

@@ -36,7 +36,8 @@ def tile_bcnnresnet_kernel(tc, feat, W, b, out):
         gwpool = ctx.enter_context(tc.tile_pool(name="gwpool", bufs=3))
         accp = ctx.enter_context(tc.psum_pool(name="accp", bufs=1))
         tps = ctx.enter_context(tc.psum_pool(name="tps", bufs=5))
-        wps = ctx.enter_context(tc.psum_pool(name="wps", bufs=2))
+        wps = ctx.enter_context(tc.psum_pool(name="wps", bufs=1))
+        dps = ctx.enter_context(tc.psum_pool(name="dps", bufs=1))
 
         F = const.tile([P, NG, D], BF16, name="F")
         feat_v = feat.rearrange("(g nl) j -> nl g j", nl=NL)
@@ -131,6 +132,7 @@ def tile_bcnnresnet_kernel(tc, feat, W, b, out):
         )
 
         acc = accp.tile([P, B], F32, name="acc")
+        idle = dps.tile([P, B], F32, name="idle")
 
         z_tiles, x_tiles, t_tiles, wq_tiles, xq_tiles = {}, {}, {}, {}, {}
 
@@ -183,18 +185,20 @@ def tile_bcnnresnet_kernel(tc, feat, W, b, out):
             nc.vector.quantize_mx(out=Xc[:].bitcast(FP8X4), scales=Xs[:], in_=G[:])
             xq_tiles[(m, J)] = (Xc, Xs)
 
-        def stage_mx(m, J):
+        def stage_mx(m, J, real, repeats):
             Wc, Ws = wq_tiles[m]
-            Xc, Xs = xq_tiles.pop((m, J))
-            nc.tensor.matmul_mx(
-                out=acc[:],
-                lhsT=Wc[:, J * P:(J + 1) * P].bitcast(FP8X4),
-                lhsT_scale=Ws[:, J * P:(J + 1) * P],
-                rhs=Xc[:].bitcast(FP8X4),
-                rhs_scale=Xs[:],
-                start=(m == 0 and J == 0),
-                stop=(m == NM - 1 and J == 1),
-            )
+            Xc, Xs = xq_tiles[(m, J)]
+            for r in range((1 if real else 0) + repeats):
+                first = real and r == 0
+                nc.tensor.matmul_mx(
+                    out=acc[:] if first else idle[:],
+                    lhsT=Wc[:, J * P:(J + 1) * P].bitcast(FP8X4),
+                    lhsT_scale=Ws[:, J * P:(J + 1) * P],
+                    rhs=Xc[:].bitcast(FP8X4),
+                    rhs_scale=Xs[:],
+                    start=(m == 0 and J == 0) if first else True,
+                    stop=(m == NM - 1 and J == 1) if first else True,
+                )
 
         stage_sqrt(0)
         stage_sqrt(1)
@@ -207,16 +211,20 @@ def tile_bcnnresnet_kernel(tc, feat, W, b, out):
                 stage_sqrt(m + 2)
             if m + 1 < NM:
                 stage_sign_i(m + 1)
-                stage_w(m + 1)
             stage_t(m, 0)
+            if m > 0:
+                stage_mx(m - 1, 0, True, 1)
             stage_t(m, 1)
             if m > 0:
-                stage_mx(m - 1, 0)
-                stage_mx(m - 1, 1)
+                stage_mx(m - 1, 1, True, 1)
+            if m + 1 < NM:
+                stage_w(m + 1)
+            if m > 0:
+                stage_mx(m - 1, 1, False, 2)
             stage_q(m, 0)
             stage_q(m, 1)
-        stage_mx(NM - 1, 0)
-        stage_mx(NM - 1, 1)
+        stage_mx(NM - 1, 0, True, 0)
+        stage_mx(NM - 1, 1, True, 0)
 
         accS = const.tile([P, B], F32, name="accS")
         nc.vector.tensor_copy(out=accS[:], in_=acc[:])

@@ -159,7 +159,7 @@ def tile_bcnnresnet_kernel(tc, feat, W, b, out):
                     o = (J * PACK + gc) * P
                     nc.tensor.transpose(out=ps[:, o:o + P], in_=Wp[:, gc, m % MM, J * P:(J + 1) * P], identity=ident_bf[:])
             Gw = gwpool.tile([P, 8 * P], BF16, name="Gw", align_bytes=64)
-            nc.scalar.copy(out=Gw[:], in_=ps[:])
+            nc.vector.tensor_copy(out=Gw[:], in_=ps[:])
             Wc = gwpool.tile([P, 2 * P], U32, name="Wc", align_bytes=64)
             Ws = gwpool.tile([P, 2 * P], U8, name="Ws", align_bytes=64)
             nc.vector.quantize_mx(out=Wc[:].bitcast(FP8X4), scales=Ws[:], in_=Gw[:])

@@ -33,7 +33,7 @@ def tile_bcnnresnet_kernel(tc, feat, W, b, out):
         gpool = ctx.enter_context(tc.tile_pool(name="gpool", bufs=4))
         cpool = ctx.enter_context(tc.tile_pool(name="cpool", bufs=4))
         wpool = ctx.enter_context(tc.tile_pool(name="wpool", bufs=3))
-        gwpool = ctx.enter_context(tc.tile_pool(name="gwpool", bufs=3))
+        gwpool = ctx.enter_context(tc.tile_pool(name="gwpool", bufs=4))
         accp = ctx.enter_context(tc.psum_pool(name="accp", bufs=1))
         tps = ctx.enter_context(tc.psum_pool(name="tps", bufs=5))
         wps = ctx.enter_context(tc.psum_pool(name="wps", bufs=1))
@@ -41,9 +41,13 @@ def tile_bcnnresnet_kernel(tc, feat, W, b, out):
 
         F = const.tile([P, NG, D], BF16, name="F")
         feat_v = feat.rearrange("(g nl) j -> nl g j", nl=NL)
+        Fs = const.tile([P, NG, D], BF16, name="Fs")
+        SH = D - PACK + 1
         queues = [nc.sync, nc.scalar, nc.gpsimd, nc.sync]
         for t in range(PACK):
             queues[t].dma_start(out=F[t:P:PACK, :, :], in_=feat_v)
+        for t in range(PACK):
+            queues[t].dma_start(out=Fs[t:P:PACK, :, 0:SH], in_=feat_v[:, :, t:t + SH])
         bb = const.tile([P, C], BF16, name="bb")
         nc.gpsimd.dma_start(out=bb[:], in_=b.partition_broadcast(P))
 
@@ -65,41 +69,19 @@ def tile_bcnnresnet_kernel(tc, feat, W, b, out):
         ident_f = const.tile([P, P], F32, name="ident_f")
         make_identity(nc, ident_f[:])
 
-        M4f = const.tile([P, PACK], F32, name="M4f")
-        nc.vector.tensor_reduce(out=M4f[:], in_=ident_bf[:].rearrange("q (nl t) -> q t nl", t=PACK), axis=AX.X, op=ALU.add)
-        M4 = const.tile([P, PACK], BF16, name="M4")
-        nc.vector.tensor_copy(out=M4[:], in_=M4f[:])
-
         A = const.tile([P, NG, D], BF16, name="A")
-        junk = const.tile([P, D], BF16, name="junk")
         Ssum = const.tile([P, NG], F32, name="Ssum")
         nz = const.tile([P, NG], F32, name="nz")
         for g in range(NG):
             nc.scalar.activation(out=A[:, g, :], in_=F[:, g, :], func=ACT.Abs, accum_out=Ssum[:, g:g + 1])
-        for g in range(NG):
-            nc.scalar.activation(out=junk[:], in_=A[:, g, :], func=ACT.Sign, accum_out=nz[:, g:g + 1])
-
-        prod = const.tile([P, NG * NM, PACK], BF16, name="prod")
-        nc.vector.tensor_tensor(
-            out=prod[:],
-            in0=F[:].rearrange("q g (m t) -> q (g m) t", t=PACK),
-            in1=M4[:].unsqueeze(1).to_broadcast([P, NG * NM, PACK]),
-            op=ALU.mult,
-        )
-        FI = const.tile([P, NG * NM], F32, name="FI")
-        nc.vector.tensor_reduce(out=FI[:], in_=prod[:], axis=AX.X, op=ALU.add)
+        nonzero = const.tile([P, NG, D], BF16, name="nonzero")
+        nc.vector.tensor_scalar(out=nonzero[:], in0=F[:], scalar1=0.0, scalar2=None, op0=ALU.not_equal)
+        nc.vector.tensor_reduce(out=nz[:], in_=nonzero[:], axis=AX.X, op=ALU.add)
+        FI = Fs[:, :, 0:SH:PACK]
         SI = const.tile([P, NG * NM], F32, name="SI")
-        nc.scalar.activation(out=SI[:], in_=FI[:], func=ACT.Sign)
-
-        SJT = []
-        for J in range(2):
-            sj = const.tile([P, NG * P], BF16, name="SJT%d" % J)
-            for h in range(2):
-                ps = tps.tile([P, 8 * P], BF16, name="ps", tag="t")
-                for gg in range(8):
-                    nc.tensor.transpose(out=ps[:, gg * P:(gg + 1) * P], in_=F[:, 8 * h + gg, J * P:(J + 1) * P], identity=ident_bf[:])
-                nc.scalar.activation(out=sj[:, h * 1024:(h + 1) * 1024], in_=ps[:], func=ACT.Sign)
-            SJT.append(sj)
+        nc.scalar.activation(out=SI[:].rearrange("q (g m) -> q g m", m=NM), in_=FI, func=ACT.Sign)
+        AI = const.tile([P, NG * NM], F32, name="AI")
+        nc.scalar.activation(out=AI[:].rearrange("q (g m) -> q g m", m=NM), in_=FI, func=ACT.Abs)
 
         def small(name):
             return const.tile([P, NG], F32, name=name)
@@ -121,8 +103,6 @@ def tile_bcnnresnet_kernel(tc, feat, W, b, out):
         nc.vector.tensor_tensor(out=rn2[:], in0=rn[:], in1=rn[:], op=ALU.mult)
         nc.vector.tensor_scalar(out=beta[:], in0=rn2[:], scalar1=EPS_SQRT, scalar2=None, op0=ALU.mult)
 
-        AI = const.tile([P, NG * NM], F32, name="AI")
-        nc.vector.tensor_tensor(out=AI[:], in0=FI[:], in1=SI[:], op=ALU.mult)
         alpha = const.tile([P, NG * NM], F32, name="alpha")
         nc.vector.tensor_tensor(
             out=alpha[:].rearrange("q (g m) -> q g m", m=NM),
@@ -134,58 +114,85 @@ def tile_bcnnresnet_kernel(tc, feat, W, b, out):
         acc = accp.tile([P, B], F32, name="acc")
         idle = dps.tile([P, B], F32, name="idle")
 
-        z_tiles, x_tiles, t_tiles, wq_tiles, xq_tiles = {}, {}, {}, {}, {}
+        z_tiles, x_tiles, t_tiles, g_tiles, wt_tiles, gw_tiles, wq_tiles, xq_tiles = {}, {}, {}, {}, {}, {}, {}, {}
+        SJT = [const.tile([P, NG * P], BF16, name="SJT%d" % J) for J in range(2)]
+
+        def stage_sjt(J, h):
+            ps = tps.tile([P, 8 * P], BF16, name="ps", tag="t")
+            for gg in range(8):
+                nc.tensor.transpose(out=ps[:, gg * P:(gg + 1) * P], in_=F[:, 8 * h + gg, J * P:(J + 1) * P], identity=ident_bf[:])
+            nc.scalar.activation(out=SJT[J][:, h * 1024:(h + 1) * 1024], in_=ps[:], func=ACT.Sign)
 
         def stage_sqrt(m):
+            if m >= NM:
+                return
             Z = zpool.tile([P, NG, D], BF16, name="Z")
             for g in range(NG):
                 col = g * NM + m
                 nc.scalar.activation(out=Z[:, g, :], in_=A[:, g, :], func=ACT.Sqrt, bias=beta[:, g:g + 1], scale=alpha[:, col:col + 1])
             z_tiles[m] = Z
 
-        def stage_sign_i(m):
-            Z = z_tiles.pop(m)
-            X = xpool.tile([P, NG, D], BF16, name="X")
-            for g in range(NG):
+        def stage_sign_i(m, h):
+            if m >= NM:
+                return
+            if h == 0:
+                x_tiles[m] = xpool.tile([P, NG, D], BF16, name="X")
+            Z, X = z_tiles[m], x_tiles[m]
+            for g in range(8 * h, 8 * h + 8):
                 col = g * NM + m
                 nc.vector.tensor_scalar(out=X[:, g, :], in0=Z[:, g, :], scalar1=SI[:, col:col + 1], scalar2=None, op0=ALU.mult)
-            x_tiles[m] = X
 
-        def stage_w(m):
+        def stage_wt(m):
+            if m >= NM:
+                return
             Wp = w_tiles[m // MM]
             ps = wps.tile([P, 8 * P], BF16, name="wt")
             for J in range(2):
                 for gc in range(PACK):
                     o = (J * PACK + gc) * P
                     nc.tensor.transpose(out=ps[:, o:o + P], in_=Wp[:, gc, m % MM, J * P:(J + 1) * P], identity=ident_bf[:])
+            wt_tiles[m] = ps
+
+        def stage_wc(m):
+            if m >= NM:
+                return
             Gw = gwpool.tile([P, 8 * P], BF16, name="Gw", align_bytes=64)
-            nc.vector.tensor_copy(out=Gw[:], in_=ps[:])
+            nc.vector.tensor_copy(out=Gw[:], in_=wt_tiles.pop(m)[:])
+            gw_tiles[m] = Gw
+
+        def stage_wq(m):
+            if m >= NM:
+                return
             Wc = gwpool.tile([P, 2 * P], U32, name="Wc", align_bytes=64)
             Ws = gwpool.tile([P, 2 * P], U8, name="Ws", align_bytes=64)
-            nc.vector.quantize_mx(out=Wc[:].bitcast(FP8X4), scales=Ws[:], in_=Gw[:])
+            nc.vector.quantize_mx(out=Wc[:].bitcast(FP8X4), scales=Ws[:], in_=gw_tiles.pop(m)[:])
             wq_tiles[m] = (Wc, Ws)
 
         def stage_t(m, J):
+            if m >= NM:
+                return
             X = x_tiles[m]
-            pss = []
             for h in range(2):
                 ps = tps.tile([P, 8 * P], BF16, name="ps", tag="t")
                 for gg in range(8):
                     nc.tensor.transpose(out=ps[:, gg * P:(gg + 1) * P], in_=X[:, 8 * h + gg, J * P:(J + 1) * P], identity=ident_bf[:])
-                pss.append(ps)
-            t_tiles[(m, J)] = pss
+                t_tiles[(m, J, h)] = ps
 
-        def stage_q(m, J):
-            pss = t_tiles.pop((m, J))
+        def stage_e(m, J):
             G = gpool.tile([P, NG * P], BF16, name="G", align_bytes=64)
             for h in range(2):
-                nc.vector.tensor_tensor(out=G[:, h * 1024:(h + 1) * 1024], in0=pss[h][:], in1=SJT[J][:, h * 1024:(h + 1) * 1024], op=ALU.mult)
+                nc.vector.tensor_tensor(out=G[:, h * 1024:(h + 1) * 1024], in0=t_tiles.pop((m, J, h))[:], in1=SJT[J][:, h * 1024:(h + 1) * 1024], op=ALU.mult)
+            g_tiles[(m, J)] = G
+
+        def stage_q(m, J):
             Xc = cpool.tile([P, B], U32, name="Xc", align_bytes=64)
             Xs = cpool.tile([P, B], U8, name="Xs", align_bytes=64)
-            nc.vector.quantize_mx(out=Xc[:].bitcast(FP8X4), scales=Xs[:], in_=G[:])
+            nc.vector.quantize_mx(out=Xc[:].bitcast(FP8X4), scales=Xs[:], in_=g_tiles.pop((m, J))[:])
             xq_tiles[(m, J)] = (Xc, Xs)
 
         def stage_mx(m, J, real, repeats):
+            if m < 0:
+                return
             Wc, Ws = wq_tiles[m]
             Xc, Xs = xq_tiles[(m, J)]
             for r in range((1 if real else 0) + repeats):
@@ -200,28 +207,40 @@ def tile_bcnnresnet_kernel(tc, feat, W, b, out):
                     stop=(m == NM - 1 and J == 1) if first else True,
                 )
 
+        ctx.enter_context(tc.manual_schedule())
         stage_sqrt(0)
         stage_sqrt(1)
-        stage_sign_i(0)
-        stage_w(0)
+        for J in range(2):
+            for h in range(2):
+                stage_sjt(J, h)
+        stage_sqrt(2)
+        stage_wt(0)
+        stage_wc(0)
+        stage_sign_i(0, 0)
+        stage_wq(0)
+        stage_wt(1)
+        stage_sign_i(0, 1)
+        stage_t(0, 0)
+        stage_t(0, 1)
+        stage_sign_i(1, 0)
+        stage_sign_i(1, 1)
         for m in range(NM):
             if m % MM == 0 and m // MM + 2 < NM // MM:
                 load_w(m // MM + 2)
-            if m + 2 < NM:
-                stage_sqrt(m + 2)
-            if m + 1 < NM:
-                stage_sign_i(m + 1)
-            stage_t(m, 0)
-            if m > 0:
-                stage_mx(m - 1, 0, True, 1)
-            stage_t(m, 1)
-            if m > 0:
-                stage_mx(m - 1, 1, True, 1)
-            if m + 1 < NM:
-                stage_w(m + 1)
-            if m > 0:
-                stage_mx(m - 1, 1, False, 2)
+            stage_sqrt(m + 3)
+            stage_wc(m + 1)
+            stage_mx(m - 1, 0, True, 1)
+            stage_wt(m + 2)
+            stage_e(m, 0)
+            stage_t(m + 1, 0)
+            stage_wq(m + 1)
+            stage_sign_i(m + 2, 0)
             stage_q(m, 0)
+            stage_mx(m - 1, 1, True, 1)
+            stage_e(m, 1)
+            stage_t(m + 1, 1)
+            stage_mx(m - 1, 1, False, 2)
+            stage_sign_i(m + 2, 1)
             stage_q(m, 1)
         stage_mx(NM - 1, 0, True, 0)
         stage_mx(NM - 1, 1, True, 0)

@@ -153,11 +153,14 @@ def tile_bcnnresnet_kernel(tc, feat, W, b, out):
                     nc.tensor.transpose(out=ps[:, o:o + P], in_=Wp[:, gc, m % MM, J * P:(J + 1) * P], identity=ident_bf[:])
             wt_tiles[m] = ps
 
-        def stage_wc(m):
-            if m >= NM:
+        def stage_wc(m, on_scalar):
+            if m >= NM or (m % 2 == 1) != on_scalar:
                 return
             Gw = gwpool.tile([P, 8 * P], BF16, name="Gw", align_bytes=64)
-            nc.vector.tensor_copy(out=Gw[:], in_=wt_tiles.pop(m)[:])
+            if on_scalar:
+                nc.scalar.copy(out=Gw[:], in_=wt_tiles.pop(m)[:])
+            else:
+                nc.vector.tensor_copy(out=Gw[:], in_=wt_tiles.pop(m)[:])
             gw_tiles[m] = Gw
 
         def stage_wq(m):
@@ -215,10 +218,11 @@ def tile_bcnnresnet_kernel(tc, feat, W, b, out):
                 stage_sjt(J, h)
         stage_sqrt(2)
         stage_wt(0)
-        stage_wc(0)
+        stage_wc(0, False)
         stage_sign_i(0, 0)
         stage_wq(0)
         stage_wt(1)
+        stage_wc(1, True)
         stage_sign_i(0, 1)
         stage_t(0, 0)
         stage_t(0, 1)
@@ -228,9 +232,10 @@ def tile_bcnnresnet_kernel(tc, feat, W, b, out):
             if m % MM == 0 and m // MM + 2 < NM // MM:
                 load_w(m // MM + 2)
             stage_sqrt(m + 3)
-            stage_wc(m + 1)
+            stage_wc(m + 1, False)
             stage_mx(m - 1, 0, True, 1)
             stage_wt(m + 2)
+            stage_wc(m + 2, True)
             stage_e(m, 0)
             stage_t(m + 1, 0)
             stage_wq(m + 1)

@@ -43,7 +43,7 @@ def tile_bcnnresnet_kernel(tc, feat, W, b, out):
         feat_v = feat.rearrange("(g nl) j -> nl g j", nl=NL)
         Fs = const.tile([P, NG, D], BF16, name="Fs")
         SH = D - PACK + 1
-        queues = [nc.sync, nc.scalar, nc.gpsimd, nc.sync]
+        queues = [nc.sync, nc.scalar, nc.sync, nc.scalar]
         for t in range(PACK):
             queues[t].dma_start(out=F[t:P:PACK, :, :], in_=feat_v)
         for t in range(PACK):
@@ -69,19 +69,15 @@ def tile_bcnnresnet_kernel(tc, feat, W, b, out):
         ident_f = const.tile([P, P], F32, name="ident_f")
         make_identity(nc, ident_f[:])
 
+        HG = NG // 2
         A = const.tile([P, NG, D], BF16, name="A")
         Ssum = const.tile([P, NG], F32, name="Ssum")
         nz = const.tile([P, NG], F32, name="nz")
-        for g in range(NG):
-            nc.scalar.activation(out=A[:, g, :], in_=F[:, g, :], func=ACT.Abs, accum_out=Ssum[:, g:g + 1])
         nonzero = const.tile([P, NG, D], BF16, name="nonzero")
-        nc.vector.tensor_scalar(out=nonzero[:], in0=F[:], scalar1=0.0, scalar2=None, op0=ALU.not_equal)
-        nc.vector.tensor_reduce(out=nz[:], in_=nonzero[:], axis=AX.X, op=ALU.add)
         FI = Fs[:, :, 0:SH:PACK]
         SI = const.tile([P, NG * NM], F32, name="SI")
-        nc.scalar.activation(out=SI[:].rearrange("q (g m) -> q g m", m=NM), in_=FI, func=ACT.Sign)
         AI = const.tile([P, NG * NM], F32, name="AI")
-        nc.scalar.activation(out=AI[:].rearrange("q (g m) -> q g m", m=NM), in_=FI, func=ACT.Abs)
+        alpha = const.tile([P, NG * NM], F32, name="alpha")
 
         def small(name):
             return const.tile([P, NG], F32, name=name)
@@ -89,27 +85,39 @@ def tile_bcnnresnet_kernel(tc, feat, W, b, out):
         sq, nq, nqe, n2, nrm, nrc, rn0, r2, hh, hn, rn, rn2, beta = [
             small(n) for n in ("sq", "nq", "nqe", "n2", "nrm", "nrc", "rn0", "r2", "hh", "hn", "rn", "rn2", "beta")
         ]
-        nc.vector.tensor_tensor(out=sq[:], in0=Ssum[:], in1=Ssum[:], op=ALU.mult)
-        nc.vector.tensor_tensor(out=nq[:], in0=nz[:], in1=nz[:], op=ALU.mult)
-        nc.vector.tensor_scalar(out=nqe[:], in0=nq[:], scalar1=EPS_SQRT, scalar2=None, op0=ALU.mult)
-        nc.vector.tensor_tensor(out=n2[:], in0=sq[:], in1=nqe[:], op=ALU.add)
-        nc.scalar.activation(out=nrm[:], in_=n2[:], func=ACT.Sqrt)
-        nc.vector.tensor_scalar(out=nrc[:], in0=nrm[:], scalar1=EPS_NORM, scalar2=None, op0=ALU.max)
-        nc.vector.reciprocal(out=rn0[:], in_=nrc[:])
-        nc.vector.tensor_tensor(out=r2[:], in0=rn0[:], in1=rn0[:], op=ALU.mult)
-        nc.vector.tensor_tensor(out=hh[:], in0=r2[:], in1=n2[:], op=ALU.mult)
-        nc.vector.tensor_scalar(out=hn[:], in0=hh[:], scalar1=-0.5, scalar2=1.5, op0=ALU.mult, op1=ALU.add)
-        nc.vector.tensor_tensor(out=rn[:], in0=rn0[:], in1=hn[:], op=ALU.mult)
-        nc.vector.tensor_tensor(out=rn2[:], in0=rn[:], in1=rn[:], op=ALU.mult)
-        nc.vector.tensor_scalar(out=beta[:], in0=rn2[:], scalar1=EPS_SQRT, scalar2=None, op0=ALU.mult)
-
-        alpha = const.tile([P, NG * NM], F32, name="alpha")
-        nc.vector.tensor_tensor(
-            out=alpha[:].rearrange("q (g m) -> q g m", m=NM),
-            in0=AI[:].rearrange("q (g m) -> q g m", m=NM),
-            in1=rn2[:].unsqueeze(2).to_broadcast([P, NG, NM]),
-            op=ALU.mult,
-        )
+        for h in range(2):
+            gs = slice(h * HG, (h + 1) * HG)
+            for g in range(h * HG, (h + 1) * HG):
+                nc.scalar.activation(out=A[:, g, :], in_=F[:, g, :], func=ACT.Abs, accum_out=Ssum[:, g:g + 1])
+            nc.vector.tensor_scalar(out=nonzero[:, gs, :], in0=F[:, gs, :], scalar1=0.0, scalar2=None, op0=ALU.not_equal)
+            nc.vector.tensor_reduce(out=nz[:, gs], in_=nonzero[:, gs, :], axis=AX.X, op=ALU.add)
+        for h in range(2):
+            gs = slice(h * HG, (h + 1) * HG)
+            cs = slice(h * HG * NM, (h + 1) * HG * NM)
+            nc.scalar.activation(out=AI[:, cs].rearrange("q (g m) -> q g m", m=NM), in_=FI[:, gs, :], func=ACT.Abs)
+            nc.scalar.activation(out=SI[:, cs].rearrange("q (g m) -> q g m", m=NM), in_=FI[:, gs, :], func=ACT.Sign)
+        for h in range(2):
+            gs = slice(h * HG, (h + 1) * HG)
+            cs = slice(h * HG * NM, (h + 1) * HG * NM)
+            nc.vector.tensor_tensor(out=sq[:, gs], in0=Ssum[:, gs], in1=Ssum[:, gs], op=ALU.mult)
+            nc.vector.tensor_tensor(out=nq[:, gs], in0=nz[:, gs], in1=nz[:, gs], op=ALU.mult)
+            nc.vector.tensor_scalar(out=nqe[:, gs], in0=nq[:, gs], scalar1=EPS_SQRT, scalar2=None, op0=ALU.mult)
+            nc.vector.tensor_tensor(out=n2[:, gs], in0=sq[:, gs], in1=nqe[:, gs], op=ALU.add)
+            nc.scalar.activation(out=nrm[:, gs], in_=n2[:, gs], func=ACT.Sqrt)
+            nc.vector.tensor_scalar(out=nrc[:, gs], in0=nrm[:, gs], scalar1=EPS_NORM, scalar2=None, op0=ALU.max)
+            nc.vector.reciprocal(out=rn0[:, gs], in_=nrc[:, gs])
+            nc.vector.tensor_tensor(out=r2[:, gs], in0=rn0[:, gs], in1=rn0[:, gs], op=ALU.mult)
+            nc.vector.tensor_tensor(out=hh[:, gs], in0=r2[:, gs], in1=n2[:, gs], op=ALU.mult)
+            nc.vector.tensor_scalar(out=hn[:, gs], in0=hh[:, gs], scalar1=-0.5, scalar2=1.5, op0=ALU.mult, op1=ALU.add)
+            nc.vector.tensor_tensor(out=rn[:, gs], in0=rn0[:, gs], in1=hn[:, gs], op=ALU.mult)
+            nc.vector.tensor_tensor(out=rn2[:, gs], in0=rn[:, gs], in1=rn[:, gs], op=ALU.mult)
+            nc.vector.tensor_scalar(out=beta[:, gs], in0=rn2[:, gs], scalar1=EPS_SQRT, scalar2=None, op0=ALU.mult)
+            nc.vector.tensor_tensor(
+                out=alpha[:, cs].rearrange("q (g m) -> q g m", m=NM),
+                in0=AI[:, cs].rearrange("q (g m) -> q g m", m=NM),
+                in1=rn2[:, gs].unsqueeze(2).to_broadcast([P, HG, NM]),
+                op=ALU.mult,
+            )
 
         acc = accp.tile([P, B], F32, name="acc")
         idle = dps.tile([P, B], F32, name="idle")
@@ -154,7 +162,7 @@ def tile_bcnnresnet_kernel(tc, feat, W, b, out):
             wt_tiles[m] = ps
 
         def stage_wc(m, on_scalar):
-            if m >= NM or (m % 2 == 1) != on_scalar:
+            if m >= NM or (m % 8 in (1, 3, 5)) != on_scalar:
                 return
             Gw = gwpool.tile([P, 8 * P], BF16, name="Gw", align_bytes=64)
             if on_scalar:
@@ -238,15 +246,15 @@ def tile_bcnnresnet_kernel(tc, feat, W, b, out):
             stage_wc(m + 2, True)
             stage_e(m, 0)
             stage_t(m + 1, 0)
-            stage_wq(m + 1)
-            stage_sign_i(m + 2, 0)
-            stage_q(m, 0)
             stage_mx(m - 1, 1, True, 1)
             stage_e(m, 1)
             stage_t(m + 1, 1)
             stage_mx(m - 1, 1, False, 2)
-            stage_sign_i(m + 2, 1)
+            stage_wq(m + 1)
+            stage_q(m, 0)
+            stage_sign_i(m + 2, 0)
             stage_q(m, 1)
+            stage_sign_i(m + 2, 1)
         stage_mx(NM - 1, 0, True, 0)
         stage_mx(NM - 1, 1, True, 0)
 

@@ -162,7 +162,7 @@ def tile_bcnnresnet_kernel(tc, feat, W, b, out):
             wt_tiles[m] = ps
 
         def stage_wc(m, on_scalar):
-            if m >= NM or (m % 8 in (1, 3, 5)) != on_scalar:
+            if m >= NM or (m % 2 == 1) != on_scalar:
                 return
             Gw = gwpool.tile([P, 8 * P], BF16, name="Gw", align_bytes=64)
             if on_scalar:
@@ -179,21 +179,22 @@ def tile_bcnnresnet_kernel(tc, feat, W, b, out):
             nc.vector.quantize_mx(out=Wc[:].bitcast(FP8X4), scales=Ws[:], in_=gw_tiles.pop(m)[:])
             wq_tiles[m] = (Wc, Ws)
 
-        def stage_t(m, J):
+        def stage_t(m, h):
             if m >= NM:
                 return
             X = x_tiles[m]
-            for h in range(2):
+            for J in range(2):
                 ps = tps.tile([P, 8 * P], BF16, name="ps", tag="t")
                 for gg in range(8):
                     nc.tensor.transpose(out=ps[:, gg * P:(gg + 1) * P], in_=X[:, 8 * h + gg, J * P:(J + 1) * P], identity=ident_bf[:])
                 t_tiles[(m, J, h)] = ps
 
-        def stage_e(m, J):
-            G = gpool.tile([P, NG * P], BF16, name="G", align_bytes=64)
-            for h in range(2):
+        def stage_e(m, h):
+            for J in range(2):
+                if h == 0:
+                    g_tiles[(m, J)] = gpool.tile([P, NG * P], BF16, name="G", align_bytes=64)
+                G = g_tiles[(m, J)]
                 nc.vector.tensor_tensor(out=G[:, h * 1024:(h + 1) * 1024], in0=t_tiles.pop((m, J, h))[:], in1=SJT[J][:, h * 1024:(h + 1) * 1024], op=ALU.mult)
-            g_tiles[(m, J)] = G
 
         def stage_q(m, J):
             Xc = cpool.tile([P, B], U32, name="Xc", align_bytes=64)
@@ -220,41 +221,38 @@ def tile_bcnnresnet_kernel(tc, feat, W, b, out):
 
         ctx.enter_context(tc.manual_schedule())
         stage_sqrt(0)
-        stage_sqrt(1)
-        for J in range(2):
-            for h in range(2):
+        for h in range(2):
+            for J in range(2):
                 stage_sjt(J, h)
-        stage_sqrt(2)
+        stage_sqrt(1)
         stage_wt(0)
         stage_wc(0, False)
         stage_sign_i(0, 0)
         stage_wq(0)
+        stage_t(0, 0)
         stage_wt(1)
         stage_wc(1, True)
         stage_sign_i(0, 1)
-        stage_t(0, 0)
         stage_t(0, 1)
-        stage_sign_i(1, 0)
-        stage_sign_i(1, 1)
         for m in range(NM):
             if m % MM == 0 and m // MM + 2 < NM // MM:
                 load_w(m // MM + 2)
-            stage_sqrt(m + 3)
-            stage_wc(m + 1, False)
+            stage_sqrt(m + 2)
             stage_mx(m - 1, 0, True, 1)
-            stage_wt(m + 2)
-            stage_wc(m + 2, True)
             stage_e(m, 0)
+            stage_sign_i(m + 1, 0)
             stage_t(m + 1, 0)
             stage_mx(m - 1, 1, True, 1)
-            stage_e(m, 1)
-            stage_t(m + 1, 1)
+            stage_wc(m + 1, False)
+            stage_wt(m + 2)
+            stage_wc(m + 2, True)
             stage_mx(m - 1, 1, False, 2)
+            stage_e(m, 1)
             stage_wq(m + 1)
             stage_q(m, 0)
-            stage_sign_i(m + 2, 0)
+            stage_sign_i(m + 1, 1)
+            stage_t(m + 1, 1)
             stage_q(m, 1)
-            stage_sign_i(m + 2, 1)
         stage_mx(NM - 1, 0, True, 0)
         stage_mx(NM - 1, 1, True, 0)
 

@@ -179,22 +179,21 @@ def tile_bcnnresnet_kernel(tc, feat, W, b, out):
             nc.vector.quantize_mx(out=Wc[:].bitcast(FP8X4), scales=Ws[:], in_=gw_tiles.pop(m)[:])
             wq_tiles[m] = (Wc, Ws)
 
-        def stage_t(m, h):
+        def stage_t(m, J):
             if m >= NM:
                 return
             X = x_tiles[m]
-            for J in range(2):
+            for h in range(2):
                 ps = tps.tile([P, 8 * P], BF16, name="ps", tag="t")
                 for gg in range(8):
                     nc.tensor.transpose(out=ps[:, gg * P:(gg + 1) * P], in_=X[:, 8 * h + gg, J * P:(J + 1) * P], identity=ident_bf[:])
                 t_tiles[(m, J, h)] = ps
 
-        def stage_e(m, h):
-            for J in range(2):
-                if h == 0:
-                    g_tiles[(m, J)] = gpool.tile([P, NG * P], BF16, name="G", align_bytes=64)
-                G = g_tiles[(m, J)]
+        def stage_e(m, J):
+            G = gpool.tile([P, NG * P], BF16, name="G", align_bytes=64)
+            for h in range(2):
                 nc.vector.tensor_tensor(out=G[:, h * 1024:(h + 1) * 1024], in0=t_tiles.pop((m, J, h))[:], in1=SJT[J][:, h * 1024:(h + 1) * 1024], op=ALU.mult)
+            g_tiles[(m, J)] = G
 
         def stage_q(m, J):
             Xc = cpool.tile([P, B], U32, name="Xc", align_bytes=64)
@@ -221,37 +220,40 @@ def tile_bcnnresnet_kernel(tc, feat, W, b, out):
 
         ctx.enter_context(tc.manual_schedule())
         stage_sqrt(0)
-        for h in range(2):
-            for J in range(2):
-                stage_sjt(J, h)
         stage_sqrt(1)
+        for J in range(2):
+            for h in range(2):
+                stage_sjt(J, h)
+        stage_sqrt(2)
         stage_wt(0)
         stage_wc(0, False)
         stage_sign_i(0, 0)
         stage_wq(0)
-        stage_t(0, 0)
         stage_wt(1)
         stage_wc(1, True)
         stage_sign_i(0, 1)
+        stage_t(0, 0)
         stage_t(0, 1)
+        stage_sign_i(1, 0)
+        stage_sign_i(1, 1)
         for m in range(NM):
             if m % MM == 0 and m // MM + 2 < NM // MM:
                 load_w(m // MM + 2)
-            stage_sqrt(m + 2)
-            stage_mx(m - 1, 0, True, 1)
-            stage_e(m, 0)
-            stage_sign_i(m + 1, 0)
-            stage_t(m + 1, 0)
-            stage_mx(m - 1, 1, True, 1)
+            stage_sqrt(m + 3)
             stage_wc(m + 1, False)
+            stage_mx(m - 1, 0, True, 1)
             stage_wt(m + 2)
             stage_wc(m + 2, True)
-            stage_mx(m - 1, 1, False, 2)
-            stage_e(m, 1)
+            stage_e(m, 0)
+            stage_t(m + 1, 0)
             stage_wq(m + 1)
+            stage_sign_i(m + 2, 0)
             stage_q(m, 0)
-            stage_sign_i(m + 1, 1)
+            stage_mx(m - 1, 1, True, 1)
+            stage_e(m, 1)
             stage_t(m + 1, 1)
+            stage_mx(m - 1, 1, False, 2)
+            stage_sign_i(m + 2, 1)
             stage_q(m, 1)
         stage_mx(NM - 1, 0, True, 0)
         stage_mx(NM - 1, 1, True, 0)

@@ -18,9 +18,14 @@ PACK = 4
 NL = P // PACK
 NG = B // NL
 NM = D // PACK
+HD = D // 2
+HM = NM // 2
+OCT = 8
+NS = HM + 2
+CH = 4
 EPS_SQRT = 1e-10
 EPS_NORM = 1e-12
-MM = 8
+START_R, START_M = 3, 8
 FLOPS = 2 * B * D * D * C
 
 
@@ -28,242 +33,411 @@ def tile_bcnnresnet_kernel(tc, feat, W, b, out):
     nc = tc.nc
     with ExitStack() as ctx:
         const = ctx.enter_context(tc.tile_pool(name="const", bufs=1))
-        zpool = ctx.enter_context(tc.tile_pool(name="zpool", bufs=3))
-        xpool = ctx.enter_context(tc.tile_pool(name="xpool", bufs=3))
-        gpool = ctx.enter_context(tc.tile_pool(name="gpool", bufs=4))
-        cpool = ctx.enter_context(tc.tile_pool(name="cpool", bufs=4))
-        wpool = ctx.enter_context(tc.tile_pool(name="wpool", bufs=3))
-        gwpool = ctx.enter_context(tc.tile_pool(name="gwpool", bufs=4))
+        zpool = ctx.enter_context(tc.tile_pool(name="zpool", bufs=4))
+        gpool = ctx.enter_context(tc.tile_pool(name="gpool", bufs=1))
+        xapool = ctx.enter_context(tc.tile_pool(name="xapool", bufs=2))
+        wrpool = ctx.enter_context(tc.tile_pool(name="wrpool", bufs=2))
+        wgpool = ctx.enter_context(tc.tile_pool(name="wgpool", bufs=3))
+        wcpool = ctx.enter_context(tc.tile_pool(name="wcpool", bufs=3))
+        tabp = ctx.enter_context(tc.tile_pool(name="tabp", bufs=2))
+        fmp = ctx.enter_context(tc.tile_pool(name="fmp", bufs=4))
         accp = ctx.enter_context(tc.psum_pool(name="accp", bufs=1))
         tps = ctx.enter_context(tc.psum_pool(name="tps", bufs=5))
         wps = ctx.enter_context(tc.psum_pool(name="wps", bufs=1))
         dps = ctx.enter_context(tc.psum_pool(name="dps", bufs=1))
 
-        F = const.tile([P, NG, D], BF16, name="F")
         feat_v = feat.rearrange("(g nl) j -> nl g j", nl=NL)
-        Fs = const.tile([P, NG, D], BF16, name="Fs")
-        SH = D - PACK + 1
-        queues = [nc.sync, nc.scalar, nc.sync, nc.scalar]
-        for t in range(PACK):
-            queues[t].dma_start(out=F[t:P:PACK, :, :], in_=feat_v)
-        for t in range(PACK):
-            queues[t].dma_start(out=Fs[t:P:PACK, :, 0:SH], in_=feat_v[:, :, t:t + SH])
-        bb = const.tile([P, C], BF16, name="bb")
-        nc.gpsimd.dma_start(out=bb[:], in_=b.partition_broadcast(P))
-
+        feat_n = feat.rearrange("(tl n) j -> n tl j", n=P)
         W_v = W.rearrange("(gc cl) (m t j) -> t gc cl m j", cl=NL, t=PACK, j=D)
-        w_tiles = {}
+        W_n = W.rearrange("c (j i) -> j c i", i=D)
 
-        def load_w(ch):
-            Wp = wpool.tile([P, PACK, MM, D], BF16, name="Wp")
-            for gc in range(PACK):
-                for t in range(PACK):
-                    nc.sync.dma_start(out=Wp[t:P:PACK, gc, :, :], in_=W_v[t, gc, :, ch * MM:(ch + 1) * MM, :])
-            w_tiles[ch] = Wp
-
-        load_w(0)
-        load_w(1)
-
-        ident_bf = const.tile([P, P], BF16, name="ident_bf")
-        make_identity(nc, ident_bf[:])
-        ident_f = const.tile([P, P], F32, name="ident_f")
-        make_identity(nc, ident_f[:])
-
-        HG = NG // 2
         A = const.tile([P, NG, D], BF16, name="A")
-        Ssum = const.tile([P, NG], F32, name="Ssum")
-        nz = const.tile([P, NG], F32, name="nz")
-        nonzero = const.tile([P, NG, D], BF16, name="nonzero")
-        FI = Fs[:, :, 0:SH:PACK]
-        SI = const.tile([P, NG * NM], F32, name="SI")
-        AI = const.tile([P, NG * NM], F32, name="AI")
+        SI = const.tile([P, NG, HM], F32, name="SI")
+        SIp = const.tile([P, HM, NG, 2], BF16, name="SIp")
         alpha = const.tile([P, NG * NM], F32, name="alpha")
+        bb = const.tile([P, C], BF16, name="bb")
+        ident_bf = const.tile([P, P], BF16, name="ident_bf")
+        ident_f = const.tile([P, P], F32, name="ident_f")
+        T16 = const.tile([P, B, 2], BF16, name="T16")
+        Wn = const.tile([P, C, 2 * HD + 2 * OCT], BF16, name="Wn")
 
         def small(name):
             return const.tile([P, NG], F32, name=name)
 
-        sq, nq, nqe, n2, nrm, nrc, rn0, r2, hh, hn, rn, rn2, beta = [
-            small(n) for n in ("sq", "nq", "nqe", "n2", "nrm", "nrc", "rn0", "r2", "hh", "hn", "rn", "rn2", "beta")
+        Ssum, nz, sq, nq, nqe, n2, nrm, nrc, rn0, r2, hh, hn, rn, rn2, beta = [
+            small(n)
+            for n in ("Ssum", "nz", "sq", "nq", "nqe", "n2", "nrm", "nrc", "rn0", "r2", "hh", "hn", "rn", "rn2", "beta")
         ]
-        for h in range(2):
-            gs = slice(h * HG, (h + 1) * HG)
-            for g in range(h * HG, (h + 1) * HG):
-                nc.scalar.activation(out=A[:, g, :], in_=F[:, g, :], func=ACT.Abs, accum_out=Ssum[:, g:g + 1])
-            nc.vector.tensor_scalar(out=nonzero[:, gs, :], in0=F[:, gs, :], scalar1=0.0, scalar2=None, op0=ALU.not_equal)
-            nc.vector.tensor_reduce(out=nz[:, gs], in_=nonzero[:, gs, :], axis=AX.X, op=ALU.add)
-        for h in range(2):
-            gs = slice(h * HG, (h + 1) * HG)
-            cs = slice(h * HG * NM, (h + 1) * HG * NM)
-            nc.scalar.activation(out=AI[:, cs].rearrange("q (g m) -> q g m", m=NM), in_=FI[:, gs, :], func=ACT.Abs)
-            nc.scalar.activation(out=SI[:, cs].rearrange("q (g m) -> q g m", m=NM), in_=FI[:, gs, :], func=ACT.Sign)
-        for h in range(2):
-            gs = slice(h * HG, (h + 1) * HG)
-            cs = slice(h * HG * NM, (h + 1) * HG * NM)
-            nc.vector.tensor_tensor(out=sq[:, gs], in0=Ssum[:, gs], in1=Ssum[:, gs], op=ALU.mult)
-            nc.vector.tensor_tensor(out=nq[:, gs], in0=nz[:, gs], in1=nz[:, gs], op=ALU.mult)
-            nc.vector.tensor_scalar(out=nqe[:, gs], in0=nq[:, gs], scalar1=EPS_SQRT, scalar2=None, op0=ALU.mult)
-            nc.vector.tensor_tensor(out=n2[:, gs], in0=sq[:, gs], in1=nqe[:, gs], op=ALU.add)
-            nc.scalar.activation(out=nrm[:, gs], in_=n2[:, gs], func=ACT.Sqrt)
-            nc.vector.tensor_scalar(out=nrc[:, gs], in0=nrm[:, gs], scalar1=EPS_NORM, scalar2=None, op0=ALU.max)
-            nc.vector.reciprocal(out=rn0[:, gs], in_=nrc[:, gs])
-            nc.vector.tensor_tensor(out=r2[:, gs], in0=rn0[:, gs], in1=rn0[:, gs], op=ALU.mult)
-            nc.vector.tensor_tensor(out=hh[:, gs], in0=r2[:, gs], in1=n2[:, gs], op=ALU.mult)
-            nc.vector.tensor_scalar(out=hn[:, gs], in0=hh[:, gs], scalar1=-0.5, scalar2=1.5, op0=ALU.mult, op1=ALU.add)
-            nc.vector.tensor_tensor(out=rn[:, gs], in0=rn0[:, gs], in1=hn[:, gs], op=ALU.mult)
-            nc.vector.tensor_tensor(out=rn2[:, gs], in0=rn[:, gs], in1=rn[:, gs], op=ALU.mult)
-            nc.vector.tensor_scalar(out=beta[:, gs], in0=rn2[:, gs], scalar1=EPS_SQRT, scalar2=None, op0=ALU.mult)
-            nc.vector.tensor_tensor(
-                out=alpha[:, cs].rearrange("q (g m) -> q g m", m=NM),
-                in0=AI[:, cs].rearrange("q (g m) -> q g m", m=NM),
-                in1=rn2[:, gs].unsqueeze(2).to_broadcast([P, HG, NM]),
-                op=ALU.mult,
-            )
 
+        fm_tiles, wr_tiles, wp_tiles = {}, {}, {}
+
+        def load_fm(k):
+            if k > HD // OCT:
+                return
+            Fm = fmp.tile([P, B // P, HD], BF16, name="Fm")
+            lo = OCT * k
+            if k > 0:
+                hi = min(HD, lo + OCT * (k % 2))
+                nc.sync.dma_start(out=Fm[:, :, 0:hi], in_=feat_n[:, :, HD:HD + hi])
+            if lo < HD:
+                nc.sync.dma_start(out=Fm[:, :, lo:HD], in_=feat_n[:, :, lo:HD])
+            fm_tiles[k] = Fm
+
+        def load_w2(ch):
+            s0 = ch * CH
+            if s0 >= NS:
+                return
+            n = min(CH, NS - s0)
+            if s0 < HM:
+                Wr = wrpool.tile([P, PACK, CH, D], BF16, name="Wr")
+                for gc in range(PACK):
+                    for t in range(PACK):
+                        nc.sync.dma_start(out=Wr[t:P:PACK, gc, :, :], in_=W_v[t, gc, :, s0:s0 + CH, :])
+                wr_tiles[ch] = Wr
+            Wp = wrpool.tile([P, PACK, CH, HD], BF16, name="Wp")
+            lo = max(0, 2 - s0)
+            m0 = HM - 2 + s0
+            for gc in range(PACK):
+                for t in range(PACK):
+                    nc.sync.dma_start(out=Wp[t:P:PACK, gc, lo:n, :], in_=W_v[t, gc, :, m0 + lo:m0 + n, HD:D])
+            wp_tiles[ch] = Wp
+
+        def load_w1():
+            for q in range(4):
+                cs = slice(q * 32, q * 32 + 32)
+                nc.sync.dma_start(out=Wn[:, cs, 0:HD], in_=W_n[HD:D, cs, 0:HD])
+            for q in range(4):
+                cs = slice(q * 32, q * 32 + 32)
+                nc.sync.dma_start(out=Wn[:, cs, HD:D], in_=W_n[0:HD, cs, 0:HD])
+            for o in (0, 1, 2, 3, 8, 9, 10, 11, 4, 5, 6, 7, 12, 13, 14, 15):
+                ps = slice(o * OCT, (o + 1) * OCT)
+                lo = (o + 1) * OCT
+                nc.sync.dma_start(out=Wn[ps, :, HD + lo:HD + HD + OCT], in_=W_n[HD + o * OCT:HD + lo, :, HD + o * OCT:D])
+
+        with tc.tile_pool(name="pro", bufs=1) as pro:
+            F = pro.tile([P, NG, D], BF16, name="F")
+            Fs = pro.tile([P, NG, D], BF16, name="Fs")
+            nonzero = pro.tile([P, NG, D], BF16, name="nonzero")
+            AI = pro.tile([P, NG * NM], F32, name="AI")
+            SH = D - PACK + 1
+            queues = [nc.sync, nc.scalar, nc.sync, nc.scalar]
+            for t in range(PACK):
+                queues[t].dma_start(out=F[t:P:PACK, :, :], in_=feat_v)
+            for t in range(PACK):
+                queues[t].dma_start(out=Fs[t:P:PACK, :, 0:SH], in_=feat_v[:, :, t:t + SH])
+            nc.gpsimd.dma_start(out=bb[:], in_=b.partition_broadcast(P))
+            load_fm(HD // OCT)
+            load_fm(0)
+            load_w2(0)
+            load_fm(1)
+            load_fm(2)
+            load_w2(1)
+            load_w1()
+            make_identity(nc, ident_bf[:])
+            make_identity(nc, ident_f[:])
+            FI = Fs[:, :, 0:SH:PACK]
+            HG = NG // 2
+            for h in range(2):
+                gs = slice(h * HG, (h + 1) * HG)
+                for g in range(h * HG, (h + 1) * HG):
+                    nc.scalar.activation(out=A[:, g, :], in_=F[:, g, :], func=ACT.Abs, accum_out=Ssum[:, g:g + 1])
+                nc.vector.tensor_scalar(out=nonzero[:, gs, :], in0=F[:, gs, :], scalar1=0.0, scalar2=None, op0=ALU.not_equal)
+                nc.vector.tensor_reduce(out=nz[:, gs], in_=nonzero[:, gs, :], axis=AX.X, op=ALU.add)
+            for h in range(2):
+                gs = slice(h * HG, (h + 1) * HG)
+                cs = slice(h * HG * NM, (h + 1) * HG * NM)
+                nc.scalar.activation(out=AI[:, cs].rearrange("q (g m) -> q g m", m=NM), in_=FI[:, gs, :], func=ACT.Abs)
+                nc.scalar.activation(out=SI[:, gs, :], in_=FI[:, gs, 0:HM], func=ACT.Sign)
+            nc.scalar.activation(out=SIp[:], in_=FI[:, :, HM:NM].rearrange("q g m -> q m g").unsqueeze(3).to_broadcast([P, HM, NG, 2]), func=ACT.Sign)
+            for h in range(2):
+                gs = slice(h * HG, (h + 1) * HG)
+                cs = slice(h * HG * NM, (h + 1) * HG * NM)
+                nc.vector.tensor_tensor(out=sq[:, gs], in0=Ssum[:, gs], in1=Ssum[:, gs], op=ALU.mult)
+                nc.vector.tensor_tensor(out=nq[:, gs], in0=nz[:, gs], in1=nz[:, gs], op=ALU.mult)
+                nc.vector.tensor_scalar(out=nqe[:, gs], in0=nq[:, gs], scalar1=EPS_SQRT, scalar2=None, op0=ALU.mult)
+                nc.vector.tensor_tensor(out=n2[:, gs], in0=sq[:, gs], in1=nqe[:, gs], op=ALU.add)
+                nc.scalar.activation(out=nrm[:, gs], in_=n2[:, gs], func=ACT.Sqrt)
+                nc.vector.tensor_scalar(out=nrc[:, gs], in0=nrm[:, gs], scalar1=EPS_NORM, scalar2=None, op0=ALU.max)
+                nc.vector.reciprocal(out=rn0[:, gs], in_=nrc[:, gs])
+                nc.vector.tensor_tensor(out=r2[:, gs], in0=rn0[:, gs], in1=rn0[:, gs], op=ALU.mult)
+                nc.vector.tensor_tensor(out=hh[:, gs], in0=r2[:, gs], in1=n2[:, gs], op=ALU.mult)
+                nc.vector.tensor_scalar(out=hn[:, gs], in0=hh[:, gs], scalar1=-0.5, scalar2=1.5, op0=ALU.mult, op1=ALU.add)
+                nc.vector.tensor_tensor(out=rn[:, gs], in0=rn0[:, gs], in1=hn[:, gs], op=ALU.mult)
+                nc.vector.tensor_tensor(out=rn2[:, gs], in0=rn[:, gs], in1=rn[:, gs], op=ALU.mult)
+                nc.vector.tensor_scalar(out=beta[:, gs], in0=rn2[:, gs], scalar1=EPS_SQRT, scalar2=None, op0=ALU.mult)
+                nc.vector.tensor_tensor(
+                    out=alpha[:, cs].rearrange("q (g m) -> q g m", m=NM),
+                    in0=AI[:, cs].rearrange("q (g m) -> q g m", m=NM),
+                    in1=rn2[:, gs].unsqueeze(2).to_broadcast([P, HG, NM]),
+                    op=ALU.mult,
+                )
+
+        xrpool = ctx.enter_context(tc.tile_pool(name="xrpool", bufs=5))
+        xmpool = ctx.enter_context(tc.tile_pool(name="xmpool", bufs=10))
         acc = accp.tile([P, B], F32, name="acc")
         idle = dps.tile([P, B], F32, name="idle")
 
-        z_tiles, x_tiles, t_tiles, g_tiles, wt_tiles, gw_tiles, wq_tiles, xq_tiles = {}, {}, {}, {}, {}, {}, {}, {}
-        SJT = [const.tile([P, NG * P], BF16, name="SJT%d" % J) for J in range(2)]
+        z_tiles, t_tiles, g_tiles, xa_tiles, xb_tiles = {}, {}, {}, {}, {}
+        wt_tiles, wg_tiles, wq_tiles, tt_tiles, tabs = {}, {}, {}, {}, {HD // OCT: T16}
+        passes = []
+        N_PASS = 4 * HM + 2 * (NS - HM)
 
-        def stage_sjt(J, h):
+        def stage_tab_t(k):
+            if k not in fm_tiles:
+                return
+            Fm = fm_tiles.pop(k)
+            ps = tps.tile([P, B], BF16, name="pst", tag="t")
+            for tl in range(B // P):
+                nc.tensor.transpose(out=ps[:, tl * P:(tl + 1) * P], in_=Fm[:, tl, :], identity=ident_bf[:])
+            tt_tiles[k] = ps
+
+        def stage_tab_s(k):
+            if k not in tt_tiles:
+                return
+            if k not in tabs:
+                tabs[k] = tabp.tile([P, B, 2], BF16, name="T")
+            nc.scalar.activation(out=tabs[k][:], in_=tt_tiles.pop(k)[:].unsqueeze(2).to_broadcast([P, B, 2]), func=ACT.Sign)
+
+        def stage_sqrt(s, q):
+            if s >= NS:
+                return
+            if q == 0:
+                z_tiles[s] = zpool.tile([P, NG, D], BF16, name="Z")
+            Z = z_tiles[s]
+            lo = OCT * (s // 2)
+            for g in range(4 * q, 4 * q + 4):
+                if s < HM:
+                    col = g * NM + s
+                    nc.scalar.activation(out=Z[:, g, lo:D], in_=A[:, g, lo:D], func=ACT.Sqrt, bias=beta[:, g:g + 1], scale=alpha[:, col:col + 1])
+                if s >= 2:
+                    col = g * NM + HM - 2 + s
+                    nc.scalar.activation(out=Z[:, g, 0:lo], in_=A[:, g, HD:HD + lo], func=ACT.Sqrt, bias=beta[:, g:g + 1], scale=alpha[:, col:col + 1])
+
+        def stage_sign(s, q):
+            if s >= HM:
+                return
+            Z = z_tiles[s]
+            lo = OCT * (s // 2)
+            for g in range(4 * q, 4 * q + 4):
+                nc.vector.tensor_scalar(out=Z[:, g, lo:D], in0=Z[:, g, lo:D], scalar1=SI[:, g, s:s + 1], scalar2=None, op0=ALU.mult)
+
+        def stage_sign2(s):
+            if s < 2 or s >= NS:
+                return
+            lo = OCT * (s // 2)
+            V = z_tiles[s][:, :, 0:lo].rearrange("p g (h w) -> p g h w", w=2)
+            nc.vector.tensor_tensor(out=V, in0=V, in1=SIp[:, s - 2, :, :].unsqueeze(2).to_broadcast([P, NG, lo // 2, 2]), op=ALU.mult)
+
+        def stage_t(s, j):
+            if s >= NS or (s >= HM and j >= 2):
+                return
+            Z = z_tiles[s]
+            c0 = (j // 2) * HD
             ps = tps.tile([P, 8 * P], BF16, name="ps", tag="t")
             for gg in range(8):
-                nc.tensor.transpose(out=ps[:, gg * P:(gg + 1) * P], in_=F[:, 8 * h + gg, J * P:(J + 1) * P], identity=ident_bf[:])
-            nc.scalar.activation(out=SJT[J][:, h * 1024:(h + 1) * 1024], in_=ps[:], func=ACT.Sign)
+                nc.tensor.transpose(out=ps[:, gg * P:(gg + 1) * P], in_=Z[:, 8 * (j % 2) + gg, c0:c0 + HD], identity=ident_bf[:])
+            t_tiles[(s, j)] = ps
 
-        def stage_sqrt(m):
-            if m >= NM:
+        def stage_e(s, j):
+            if s >= HM and j >= 2:
                 return
-            Z = zpool.tile([P, NG, D], BF16, name="Z")
-            for g in range(NG):
-                col = g * NM + m
-                nc.scalar.activation(out=Z[:, g, :], in_=A[:, g, :], func=ACT.Sqrt, bias=beta[:, g:g + 1], scale=alpha[:, col:col + 1])
-            z_tiles[m] = Z
+            if j == 0:
+                g_tiles[s] = gpool.tile([P, 2 * NG * P], BF16, name="G", align_bytes=64)
+            T = tabs[s // 2] if j < 2 else T16
+            h = j % 2
+            nc.vector.tensor_tensor(
+                out=g_tiles[s][:, j * 1024:(j + 1) * 1024].rearrange("p (n a b) -> p n a b", a=2, b=2),
+                in0=t_tiles.pop((s, j))[:].rearrange("p (n a b) -> p n a b", a=2, b=2),
+                in1=T[:, h * 256:(h + 1) * 256, :].unsqueeze(2).to_broadcast([P, 256, 2, 2]),
+                op=ALU.mult,
+            )
 
-        def stage_sign_i(m, h):
-            if m >= NM:
-                return
-            if h == 0:
-                x_tiles[m] = xpool.tile([P, NG, D], BF16, name="X")
-            Z, X = z_tiles[m], x_tiles[m]
-            for g in range(8 * h, 8 * h + 8):
-                col = g * NM + m
-                nc.vector.tensor_scalar(out=X[:, g, :], in0=Z[:, g, :], scalar1=SI[:, col:col + 1], scalar2=None, op0=ALU.mult)
+        def stage_q(s):
+            n = 2 * B if s < HM else B
+            Xc = xapool.tile([P, 2 * B], U32, name="Xc", align_bytes=64)
+            Xs = xapool.tile([P, 2 * B], U8, name="Xs", align_bytes=64)
+            nc.vector.quantize_mx(out=Xc[:, 0:n].bitcast(FP8X4), scales=Xs[:, 0:n], in_=g_tiles[s][:, 0:PACK * n])
+            xa_tiles[s] = (Xc, Xs)
 
-        def stage_wt(m):
-            if m >= NM:
+        def stage_q2(s, h):
+            if s >= HM and h == 1:
                 return
-            Wp = w_tiles[m // MM]
+            pool = xrpool if h == 1 else xmpool
+            Xc = pool.tile([P, B], U32, name="Yc", align_bytes=64)
+            Xs = pool.tile([P, B], U8, name="Ys", align_bytes=64)
+            nc.vector.quantize_mx(out=Xc[:].bitcast(FP8X4), scales=Xs[:], in_=g_tiles[s][:, h * PACK * B:(h + 1) * PACK * B])
+            xb_tiles[(s, h)] = (Xc, Xs)
+
+        def stage_w2mix(k):
+            if k > HD // OCT:
+                return
+            s = 2 * k
+            e = slice(s % CH, s % CH + 2)
+            Wp = wp_tiles[s // CH]
+            if s >= HM:
+                nc.vector.memset(Wp[:, :, e, HD - OCT:HD], 0.0)
+                return
+            Wr = wr_tiles[s // CH]
+            lo = OCT * k
+            nc.vector.memset(Wr[:, :, e, max(0, lo - OCT):lo + OCT], 0.0)
+            if k >= 2:
+                nc.vector.tensor_copy(out=Wr[:, :, e, 0:lo - OCT], in_=Wp[:, :, e, 0:lo - OCT])
+
+        def stage_w2t(s):
+            if s >= NS:
+                return
             ps = wps.tile([P, 8 * P], BF16, name="wt")
-            for J in range(2):
+            for h in range(2 if s < HM else 1):
                 for gc in range(PACK):
-                    o = (J * PACK + gc) * P
-                    nc.tensor.transpose(out=ps[:, o:o + P], in_=Wp[:, gc, m % MM, J * P:(J + 1) * P], identity=ident_bf[:])
-            wt_tiles[m] = ps
+                    o = (h * PACK + gc) * P
+                    src = wr_tiles[s // CH] if s < HM else wp_tiles[s // CH]
+                    nc.tensor.transpose(out=ps[:, o:o + P], in_=src[:, gc, s % CH, h * HD:(h + 1) * HD], identity=ident_bf[:])
+            wt_tiles[s] = ps
 
-        def stage_wc(m, on_scalar):
-            if m >= NM or (m % 2 == 1) != on_scalar:
+        def stage_w2c(s):
+            if s >= NS:
                 return
-            Gw = gwpool.tile([P, 8 * P], BF16, name="Gw", align_bytes=64)
-            if on_scalar:
-                nc.scalar.copy(out=Gw[:], in_=wt_tiles.pop(m)[:])
-            else:
-                nc.vector.tensor_copy(out=Gw[:], in_=wt_tiles.pop(m)[:])
-            gw_tiles[m] = Gw
+            n = 8 * P if s < HM else 4 * P
+            Wg = wgpool.tile([P, 8 * P], BF16, name="Wg2", align_bytes=64)
+            nc.scalar.copy(out=Wg[:, 0:n], in_=wt_tiles.pop(s)[:, 0:n])
+            wg_tiles[(2, s)] = Wg
 
-        def stage_wq(m):
-            if m >= NM:
+        def stage_w1c(s, h):
+            Wg = wgpool.tile([P, 4 * P], BF16, name="Wg1%d" % h, align_bytes=64)
+            col = (1 - h) * (HD // 2) + 2 * s
+            src = Wn[:].bitcast(F32)[:, :, col:col + 2]
+            nc.scalar.copy(out=Wg[:].bitcast(F32).rearrange("p (c w) -> p c w", w=2), in_=src)
+            wg_tiles[(h, s)] = Wg
+
+        def stage_wq(kind, s):
+            if (kind, s) not in wg_tiles:
                 return
-            Wc = gwpool.tile([P, 2 * P], U32, name="Wc", align_bytes=64)
-            Ws = gwpool.tile([P, 2 * P], U8, name="Ws", align_bytes=64)
-            nc.vector.quantize_mx(out=Wc[:].bitcast(FP8X4), scales=Ws[:], in_=gw_tiles.pop(m)[:])
-            wq_tiles[m] = (Wc, Ws)
+            n = 2 * P if kind == 2 and s < HM else P
+            Wc = wcpool.tile([P, 2 * P if kind == 2 else P], U32, name="Wc%d" % kind, align_bytes=64)
+            Ws = wcpool.tile([P, 2 * P if kind == 2 else P], U8, name="Ws%d" % kind, align_bytes=64)
+            nc.vector.quantize_mx(out=Wc[:, 0:n].bitcast(FP8X4), scales=Ws[:, 0:n], in_=wg_tiles.pop((kind, s))[:, 0:PACK * n])
+            wq_tiles[(kind, s)] = (Wc, Ws)
 
-        def stage_t(m, J):
-            if m >= NM:
+        def mx_pass(dst, w, wcol, x, xcol, start, stop):
+            nc.tensor.matmul_mx(
+                out=dst[:],
+                lhsT=w[0][:, wcol:wcol + P].bitcast(FP8X4),
+                lhsT_scale=w[1][:, wcol:wcol + P],
+                rhs=x[0][:, xcol:xcol + B].bitcast(FP8X4),
+                rhs_scale=x[1][:, xcol:xcol + B],
+                start=start,
+                stop=stop,
+            )
+
+        def acc_pass(w, wcol, x, xcol):
+            passes.append(wcol)
+            mx_pass(acc, w, wcol, x, xcol, len(passes) == 1, len(passes) == N_PASS)
+
+        def stage_mx2(s):
+            if s < 0:
                 return
-            X = x_tiles[m]
-            for h in range(2):
-                ps = tps.tile([P, 8 * P], BF16, name="ps", tag="t")
-                for gg in range(8):
-                    nc.tensor.transpose(out=ps[:, gg * P:(gg + 1) * P], in_=X[:, 8 * h + gg, J * P:(J + 1) * P], identity=ident_bf[:])
-                t_tiles[(m, J, h)] = ps
+            for h in range(2 if s < HM else 1):
+                acc_pass(wq_tiles[(2, s)], h * P, xa_tiles[s], h * B)
 
-        def stage_e(m, J):
-            G = gpool.tile([P, NG * P], BF16, name="G", align_bytes=64)
-            for h in range(2):
-                nc.vector.tensor_tensor(out=G[:, h * 1024:(h + 1) * 1024], in0=t_tiles.pop((m, J, h))[:], in1=SJT[J][:, h * 1024:(h + 1) * 1024], op=ALU.mult)
-            g_tiles[(m, J)] = G
+        def stage_mx1(s, h):
+            acc_pass(wq_tiles[(h, s)], 0, xb_tiles[(s, h)], 0)
 
-        def stage_q(m, J):
-            Xc = cpool.tile([P, B], U32, name="Xc", align_bytes=64)
-            Xs = cpool.tile([P, B], U8, name="Xs", align_bytes=64)
-            nc.vector.quantize_mx(out=Xc[:].bitcast(FP8X4), scales=Xs[:], in_=g_tiles.pop((m, J))[:])
-            xq_tiles[(m, J)] = (Xc, Xs)
-
-        def stage_mx(m, J, real, repeats):
-            if m < 0:
+        def stage_idle(s, n):
+            if s < 0:
                 return
-            Wc, Ws = wq_tiles[m]
-            Xc, Xs = xq_tiles[(m, J)]
-            for r in range((1 if real else 0) + repeats):
-                first = real and r == 0
-                nc.tensor.matmul_mx(
-                    out=acc[:] if first else idle[:],
-                    lhsT=Wc[:, J * P:(J + 1) * P].bitcast(FP8X4),
-                    lhsT_scale=Ws[:, J * P:(J + 1) * P],
-                    rhs=Xc[:].bitcast(FP8X4),
-                    rhs_scale=Xs[:],
-                    start=(m == 0 and J == 0) if first else True,
-                    stop=(m == NM - 1 and J == 1) if first else True,
-                )
+            for r in range(n):
+                mx_pass(idle, wq_tiles[(2, s)], 0, xa_tiles[s], 0, True, True)
+
+        plan = {s: [] for s in range(NS)}
+        for h, start, n in ((1, START_R, HM), (0, START_M, NS)):
+            nxt = 0
+            for s in range(start, NS):
+                for r in range(2 if s % 3 == 2 else 1):
+                    if nxt < n and nxt <= s:
+                        plan[s].append((nxt, h))
+                        nxt += 1
 
         ctx.enter_context(tc.manual_schedule())
-        stage_sqrt(0)
-        stage_sqrt(1)
-        for J in range(2):
-            for h in range(2):
-                stage_sjt(J, h)
-        stage_sqrt(2)
-        stage_wt(0)
-        stage_wc(0, False)
-        stage_sign_i(0, 0)
-        stage_wq(0)
-        stage_wt(1)
-        stage_wc(1, True)
-        stage_sign_i(0, 1)
-        stage_t(0, 0)
-        stage_t(0, 1)
-        stage_sign_i(1, 0)
-        stage_sign_i(1, 1)
-        for m in range(NM):
-            if m % MM == 0 and m // MM + 2 < NM // MM:
-                load_w(m // MM + 2)
-            stage_sqrt(m + 3)
-            stage_wc(m + 1, False)
-            stage_mx(m - 1, 0, True, 1)
-            stage_wt(m + 2)
-            stage_wc(m + 2, True)
-            stage_e(m, 0)
-            stage_t(m + 1, 0)
-            stage_wq(m + 1)
-            stage_sign_i(m + 2, 0)
-            stage_q(m, 0)
-            stage_mx(m - 1, 1, True, 1)
-            stage_e(m, 1)
-            stage_t(m + 1, 1)
-            stage_mx(m - 1, 1, False, 2)
-            stage_sign_i(m + 2, 1)
-            stage_q(m, 1)
-        stage_mx(NM - 1, 0, True, 0)
-        stage_mx(NM - 1, 1, True, 0)
+        K16 = HD // OCT
+        for q in range(4):
+            stage_sqrt(0, q)
+        stage_tab_t(K16)
+        stage_tab_t(0)
+        stage_tab_s(K16)
+        stage_tab_s(0)
+        for q in range(4):
+            stage_sqrt(1, q)
+        stage_w2mix(0)
+        stage_w2mix(1)
+        stage_w2t(0)
+        stage_w2c(0)
+        stage_w2t(1)
+        for q in range(4):
+            stage_sign(0, q)
+        for j in range(4):
+            stage_t(0, j)
+        for q in range(4):
+            stage_sqrt(2, q)
+        for q in range(4):
+            stage_sign(1, q)
+        for s in range(NS):
+            old = plan.get(s - 1, [])
+            old2 = plan.get(s - 2, [])
+            if s % 2 == 0 and s // 2 + 3 < K16:
+                load_fm(s // 2 + 3)
+            if s % CH == 2:
+                load_w2(s // CH + 2)
+            if s % 2 == 1:
+                stage_tab_s(s // 2 + 1)
+            stage_sqrt(s + 3, 0)
+            stage_w2c(s + 1)
+            stage_sqrt(s + 3, 1)
+            for w, h in plan[s]:
+                stage_w1c(w, h)
+            stage_mx2(s - 1)
+            if s % 2 == 0 and s // 2 + 1 < K16:
+                stage_tab_t(s // 2 + 1)
+            stage_e(s, 0)
+            stage_t(s + 1, 0)
+            stage_sign(s + 2, 0)
+            stage_wq(2, s)
+            stage_e(s, 1)
+            stage_t(s + 1, 1)
+            stage_idle(s - 1, 2)
+            stage_w2t(s + 2)
+            stage_sqrt(s + 3, 2)
+            stage_sqrt(s + 3, 3)
+            stage_sign(s + 2, 1)
+            stage_e(s, 2)
+            stage_sign(s + 2, 2)
+            stage_e(s, 3)
+            for w, h in old2:
+                stage_mx1(w, h)
+            stage_t(s + 1, 2)
+            stage_sign(s + 2, 3)
+            stage_sign2(s + 2)
+            stage_q(s)
+            for w, h in old:
+                stage_wq(h, w)
+            if s % 2 == 1:
+                stage_w2mix((s + 3) // 2)
+            stage_q2(s, 0)
+            stage_q2(s, 1)
+            stage_t(s + 1, 3)
+            stage_idle(s - 1, 2)
+        stage_mx2(NS - 1)
+        for w, h in plan[NS - 2]:
+            stage_mx1(w, h)
+        for w, h in plan[NS - 1]:
+            stage_wq(h, w)
+            stage_mx1(w, h)
 
-        accS = const.tile([P, B], F32, name="accS")
+        accS = zpool.tile([P, B], F32, name="Z")
         nc.vector.tensor_copy(out=accS[:], in_=acc[:])
         pso = tps.tile([P, B], F32, name="pso", tag="t")
         for nb in range(B // P):
             nc.tensor.transpose(out=pso[:, nb * P:(nb + 1) * P], in_=accS[:, nb * P:(nb + 1) * P], identity=ident_f[:])
-        res = const.tile([P, B // P, C], F32, name="res")
+        res = zpool.tile([P, B // P, C], F32, name="Z")
         nc.vector.tensor_tensor(
             out=res[:],
             in0=pso[:].rearrange("p (nb c) -> p nb c", c=C),

@@ -25,7 +25,7 @@ NS = HM + 2
 CH = 4
 EPS_SQRT = 1e-10
 EPS_NORM = 1e-12
-START_R, START_M = 3, 8
+START_R, START_M = 3, 6
 FLOPS = 2 * B * D * D * C
 
 
@@ -33,14 +33,16 @@ def tile_bcnnresnet_kernel(tc, feat, W, b, out):
     nc = tc.nc
     with ExitStack() as ctx:
         const = ctx.enter_context(tc.tile_pool(name="const", bufs=1))
-        zpool = ctx.enter_context(tc.tile_pool(name="zpool", bufs=4))
+        zpool = ctx.enter_context(tc.tile_pool(name="zpool", bufs=3))
         gpool = ctx.enter_context(tc.tile_pool(name="gpool", bufs=1))
         xapool = ctx.enter_context(tc.tile_pool(name="xapool", bufs=2))
         wrpool = ctx.enter_context(tc.tile_pool(name="wrpool", bufs=2))
         wgpool = ctx.enter_context(tc.tile_pool(name="wgpool", bufs=3))
+        wg2pool = ctx.enter_context(tc.tile_pool(name="wg2pool", bufs=2))
         wcpool = ctx.enter_context(tc.tile_pool(name="wcpool", bufs=3))
+        wc2pool = ctx.enter_context(tc.tile_pool(name="wc2pool", bufs=2))
         tabp = ctx.enter_context(tc.tile_pool(name="tabp", bufs=2))
-        fmp = ctx.enter_context(tc.tile_pool(name="fmp", bufs=4))
+        fmp = ctx.enter_context(tc.tile_pool(name="fmp", bufs=3))
         accp = ctx.enter_context(tc.psum_pool(name="accp", bufs=1))
         tps = ctx.enter_context(tc.psum_pool(name="tps", bufs=5))
         wps = ctx.enter_context(tc.psum_pool(name="wps", bufs=1))
@@ -59,7 +61,10 @@ def tile_bcnnresnet_kernel(tc, feat, W, b, out):
         ident_bf = const.tile([P, P], BF16, name="ident_bf")
         ident_f = const.tile([P, P], F32, name="ident_f")
         T16 = const.tile([P, B, 2], BF16, name="T16")
-        Wn = const.tile([P, C, 2 * HD + 2 * OCT], BF16, name="Wn")
+        Wa = const.tile([P, C, HD], BF16, name="Wa")
+        Wb = const.tile([P, C, D], BF16, name="Wb")
+        mask_a = const.tile([P, P], BF16, name="mask_a")
+        mask_b = const.tile([P, P], BF16, name="mask_b")
 
         def small(name):
             return const.tile([P, NG], F32, name=name)
@@ -102,17 +107,10 @@ def tile_bcnnresnet_kernel(tc, feat, W, b, out):
                     nc.sync.dma_start(out=Wp[t:P:PACK, gc, lo:n, :], in_=W_v[t, gc, :, m0 + lo:m0 + n, HD:D])
             wp_tiles[ch] = Wp
 
-        def load_w1():
+        def load_wn(dst, j0, n):
             for q in range(4):
                 cs = slice(q * 32, q * 32 + 32)
-                nc.sync.dma_start(out=Wn[:, cs, 0:HD], in_=W_n[HD:D, cs, 0:HD])
-            for q in range(4):
-                cs = slice(q * 32, q * 32 + 32)
-                nc.sync.dma_start(out=Wn[:, cs, HD:D], in_=W_n[0:HD, cs, 0:HD])
-            for o in (0, 1, 2, 3, 8, 9, 10, 11, 4, 5, 6, 7, 12, 13, 14, 15):
-                ps = slice(o * OCT, (o + 1) * OCT)
-                lo = (o + 1) * OCT
-                nc.sync.dma_start(out=Wn[ps, :, HD + lo:HD + HD + OCT], in_=W_n[HD + o * OCT:HD + lo, :, HD + o * OCT:D])
+                nc.sync.dma_start(out=dst[:, cs, :], in_=W_n[j0:j0 + HD, cs, 0:n])
 
         with tc.tile_pool(name="pro", bufs=1) as pro:
             F = pro.tile([P, NG, D], BF16, name="F")
@@ -130,11 +128,13 @@ def tile_bcnnresnet_kernel(tc, feat, W, b, out):
             load_fm(0)
             load_w2(0)
             load_fm(1)
-            load_fm(2)
+            load_wn(Wb, HD, D)
             load_w2(1)
-            load_w1()
+            load_wn(Wa, 0, HD)
             make_identity(nc, ident_bf[:])
             make_identity(nc, ident_f[:])
+            nc.gpsimd.tensor_copy(out=mask_a[:], in_=ident_bf[:])
+            nc.gpsimd.memset(mask_b[:], 0.0)
             FI = Fs[:, :, 0:SH:PACK]
             HG = NG // 2
             for h in range(2):
@@ -173,12 +173,12 @@ def tile_bcnnresnet_kernel(tc, feat, W, b, out):
                 )
 
         xrpool = ctx.enter_context(tc.tile_pool(name="xrpool", bufs=5))
-        xmpool = ctx.enter_context(tc.tile_pool(name="xmpool", bufs=10))
+        xmpool = ctx.enter_context(tc.tile_pool(name="xmpool", bufs=8))
         acc = accp.tile([P, B], F32, name="acc")
-        idle = dps.tile([P, B], F32, name="idle")
 
         z_tiles, t_tiles, g_tiles, xa_tiles, xb_tiles = {}, {}, {}, {}, {}
         wt_tiles, wg_tiles, wq_tiles, tt_tiles, tabs = {}, {}, {}, {}, {HD // OCT: T16}
+        mix_tiles, mask_k = {}, [0]
         passes = []
         N_PASS = 4 * HM + 2 * (NS - HM)
 
@@ -298,23 +298,60 @@ def tile_bcnnresnet_kernel(tc, feat, W, b, out):
             if s >= NS:
                 return
             n = 8 * P if s < HM else 4 * P
-            Wg = wgpool.tile([P, 8 * P], BF16, name="Wg2", align_bytes=64)
+            Wg = wg2pool.tile([P, 8 * P], BF16, name="Wg2", align_bytes=64)
             nc.scalar.copy(out=Wg[:, 0:n], in_=wt_tiles.pop(s)[:, 0:n])
             wg_tiles[(2, s)] = Wg
 
+        def mixes(s, h):
+            return h == 0 and (s // 2) % 4 != 0
+
+        def stage_mix(todo):
+            todo = [s for s, h in todo if mixes(s, h)]
+            if not todo:
+                return
+            ps = dps.tile([P, 2, 4 * P], BF16, name="mix", tag="d")
+            for n, s in enumerate(todo):
+                k = s // 2
+                while mask_k[0] < k:
+                    cs = slice(OCT * mask_k[0], OCT * (mask_k[0] + 1))
+                    nc.gpsimd.tensor_copy(out=mask_b[:, cs], in_=ident_bf[:, cs])
+                    nc.gpsimd.memset(mask_a[:, cs], 0.0)
+                    mask_k[0] += 1
+                o = ps[:, n, :].rearrange("p (c w) -> p c w", w=4)
+                nc.tensor.matmul(out=o, lhsT=mask_a[:], rhs=Wa[:, :, 4 * s:4 * s + 4], start=True, stop=False)
+                nc.tensor.matmul(out=o, lhsT=mask_b[:], rhs=Wb[:, :, HD - OCT + 4 * s:HD - OCT + 4 * s + 4], start=False, stop=True)
+                mix_tiles[s] = (ps, n)
+
         def stage_w1c(s, h):
             Wg = wgpool.tile([P, 4 * P], BF16, name="Wg1%d" % h, align_bytes=64)
-            col = (1 - h) * (HD // 2) + 2 * s
-            src = Wn[:].bitcast(F32)[:, :, col:col + 2]
-            nc.scalar.copy(out=Wg[:].bitcast(F32).rearrange("p (c w) -> p c w", w=2), in_=src)
             wg_tiles[(h, s)] = Wg
+            if mixes(s, h):
+                ps, n = mix_tiles.pop(s)
+                nc.scalar.copy(out=Wg[:], in_=ps[:, n, :])
+                return
+            dst = Wg[:].bitcast(F32).rearrange("p (c w) -> p c w", w=2)
+            Va, Vb = Wa[:].bitcast(F32), Wb[:].bitcast(F32)
+            if h == 1:
+                nc.scalar.copy(out=dst, in_=Vb[:, :, 2 * s:2 * s + 2])
+                return
+            b0 = (HD - OCT) // 2 + 2 * s
+            lo = OCT * (s // 2)
+            if lo <= HD // 2:
+                nc.scalar.copy(out=dst, in_=Va[:, :, 2 * s:2 * s + 2])
+                if lo > 0:
+                    nc.scalar.copy(out=dst[0:lo], in_=Vb[0:lo, :, b0:b0 + 2])
+            else:
+                nc.scalar.copy(out=dst, in_=Vb[:, :, b0:b0 + 2])
+                if lo < HD:
+                    nc.scalar.copy(out=dst[lo:P], in_=Va[lo:P, :, 2 * s:2 * s + 2])
 
         def stage_wq(kind, s):
             if (kind, s) not in wg_tiles:
                 return
             n = 2 * P if kind == 2 and s < HM else P
-            Wc = wcpool.tile([P, 2 * P if kind == 2 else P], U32, name="Wc%d" % kind, align_bytes=64)
-            Ws = wcpool.tile([P, 2 * P if kind == 2 else P], U8, name="Ws%d" % kind, align_bytes=64)
+            pool, cols = (wc2pool, 2 * P) if kind == 2 else (wcpool, P)
+            Wc = pool.tile([P, cols], U32, name="Wc%d" % kind, align_bytes=64)
+            Ws = pool.tile([P, cols], U8, name="Ws%d" % kind, align_bytes=64)
             nc.vector.quantize_mx(out=Wc[:, 0:n].bitcast(FP8X4), scales=Ws[:, 0:n], in_=wg_tiles.pop((kind, s))[:, 0:PACK * n])
             wq_tiles[(kind, s)] = (Wc, Ws)
 
@@ -345,6 +382,7 @@ def tile_bcnnresnet_kernel(tc, feat, W, b, out):
         def stage_idle(s, n):
             if s < 0:
                 return
+            idle = dps.tile([P, B], F32, name="idle", tag="d")
             for r in range(n):
                 mx_pass(idle, wq_tiles[(2, s)], 0, xa_tiles[s], 0, True, True)
 
@@ -352,7 +390,7 @@ def tile_bcnnresnet_kernel(tc, feat, W, b, out):
         for h, start, n in ((1, START_R, HM), (0, START_M, NS)):
             nxt = 0
             for s in range(start, NS):
-                for r in range(2 if s % 3 == 2 else 1):
+                for r in range(2 if s % 2 == 0 else 1):
                     if nxt < n and nxt <= s:
                         plan[s].append((nxt, h))
                         nxt += 1
@@ -383,8 +421,8 @@ def tile_bcnnresnet_kernel(tc, feat, W, b, out):
         for s in range(NS):
             old = plan.get(s - 1, [])
             old2 = plan.get(s - 2, [])
-            if s % 2 == 0 and s // 2 + 3 < K16:
-                load_fm(s // 2 + 3)
+            if s % 2 == 0 and s // 2 + 2 < K16:
+                load_fm(s // 2 + 2)
             if s % CH == 2:
                 load_w2(s // CH + 2)
             if s % 2 == 1:
@@ -425,6 +463,7 @@ def tile_bcnnresnet_kernel(tc, feat, W, b, out):
             stage_q2(s, 1)
             stage_t(s + 1, 3)
             stage_idle(s - 1, 2)
+            stage_mix(plan.get(s + 1, []))
         stage_mx2(NS - 1)
         for w, h in plan[NS - 2]:
             stage_mx1(w, h)

@@ -22,10 +22,10 @@ HD = D // 2
 HM = NM // 2
 OCT = 8
 NS = HM + 2
-CH = 4
+CH = 2
 EPS_SQRT = 1e-10
 EPS_NORM = 1e-12
-START_R, START_M = 3, 6
+START_R, START_M = 2, 8
 FLOPS = 2 * B * D * D * C
 
 
@@ -36,10 +36,10 @@ def tile_bcnnresnet_kernel(tc, feat, W, b, out):
         zpool = ctx.enter_context(tc.tile_pool(name="zpool", bufs=3))
         gpool = ctx.enter_context(tc.tile_pool(name="gpool", bufs=1))
         xapool = ctx.enter_context(tc.tile_pool(name="xapool", bufs=2))
-        wrpool = ctx.enter_context(tc.tile_pool(name="wrpool", bufs=2))
-        wgpool = ctx.enter_context(tc.tile_pool(name="wgpool", bufs=3))
+        wrpool = ctx.enter_context(tc.tile_pool(name="wrpool", bufs=4))
+        wgpool = ctx.enter_context(tc.tile_pool(name="wgpool", bufs=2))
         wg2pool = ctx.enter_context(tc.tile_pool(name="wg2pool", bufs=2))
-        wcpool = ctx.enter_context(tc.tile_pool(name="wcpool", bufs=3))
+        wcpool = ctx.enter_context(tc.tile_pool(name="wcpool", bufs=2))
         wc2pool = ctx.enter_context(tc.tile_pool(name="wc2pool", bufs=2))
         tabp = ctx.enter_context(tc.tile_pool(name="tabp", bufs=2))
         fmp = ctx.enter_context(tc.tile_pool(name="fmp", bufs=3))
@@ -50,7 +50,7 @@ def tile_bcnnresnet_kernel(tc, feat, W, b, out):
 
         feat_v = feat.rearrange("(g nl) j -> nl g j", nl=NL)
         feat_n = feat.rearrange("(tl n) j -> n tl j", n=P)
-        W_v = W.rearrange("(gc cl) (m t j) -> t gc cl m j", cl=NL, t=PACK, j=D)
+        W_v = W.rearrange("(gc cl) (m t j) -> t m cl gc j", cl=NL, t=PACK, j=D)
         W_n = W.rearrange("c (j i) -> j c i", i=D)
 
         A = const.tile([P, NG, D], BF16, name="A")
@@ -92,25 +92,24 @@ def tile_bcnnresnet_kernel(tc, feat, W, b, out):
             s0 = ch * CH
             if s0 >= NS:
                 return
-            n = min(CH, NS - s0)
             if s0 < HM:
                 Wr = wrpool.tile([P, PACK, CH, D], BF16, name="Wr")
-                for gc in range(PACK):
+                for e in range(CH):
                     for t in range(PACK):
-                        nc.sync.dma_start(out=Wr[t:P:PACK, gc, :, :], in_=W_v[t, gc, :, s0:s0 + CH, :])
+                        nc.sync.dma_start(out=Wr[t:P:PACK, :, e, :], in_=W_v[t, s0 + e])
                 wr_tiles[ch] = Wr
+            if s0 == 0:
+                return
             Wp = wrpool.tile([P, PACK, CH, HD], BF16, name="Wp")
-            lo = max(0, 2 - s0)
-            m0 = HM - 2 + s0
-            for gc in range(PACK):
+            for e in range(CH):
                 for t in range(PACK):
-                    nc.sync.dma_start(out=Wp[t:P:PACK, gc, lo:n, :], in_=W_v[t, gc, :, m0 + lo:m0 + n, HD:D])
+                    nc.sync.dma_start(out=Wp[t:P:PACK, :, e, :], in_=W_v[t, HM - 2 + s0 + e, :, :, HD:D])
             wp_tiles[ch] = Wp
 
-        def load_wn(dst, j0, n):
+        def load_wn(dst, j0, i0):
             for q in range(4):
                 cs = slice(q * 32, q * 32 + 32)
-                nc.sync.dma_start(out=dst[:, cs, :], in_=W_n[j0:j0 + HD, cs, 0:n])
+                nc.sync.dma_start(out=dst[:, cs, i0:i0 + HD], in_=W_n[j0:j0 + HD, cs, i0:i0 + HD])
 
         with tc.tile_pool(name="pro", bufs=1) as pro:
             F = pro.tile([P, NG, D], BF16, name="F")
@@ -128,9 +127,12 @@ def tile_bcnnresnet_kernel(tc, feat, W, b, out):
             load_fm(0)
             load_w2(0)
             load_fm(1)
-            load_wn(Wb, HD, D)
             load_w2(1)
-            load_wn(Wa, 0, HD)
+            load_wn(Wb, HD, 0)
+            load_w2(2)
+            load_w2(3)
+            load_wn(Wb, HD, HD)
+            load_wn(Wa, 0, 0)
             make_identity(nc, ident_bf[:])
             make_identity(nc, ident_f[:])
             nc.gpsimd.tensor_copy(out=mask_a[:], in_=ident_bf[:])
@@ -172,8 +174,8 @@ def tile_bcnnresnet_kernel(tc, feat, W, b, out):
                     op=ALU.mult,
                 )
 
-        xrpool = ctx.enter_context(tc.tile_pool(name="xrpool", bufs=5))
-        xmpool = ctx.enter_context(tc.tile_pool(name="xmpool", bufs=8))
+        xrpool = ctx.enter_context(tc.tile_pool(name="xrpool", bufs=4))
+        xmpool = ctx.enter_context(tc.tile_pool(name="xmpool", bufs=10))
         acc = accp.tile([P, B], F32, name="acc")
 
         z_tiles, t_tiles, g_tiles, xa_tiles, xb_tiles = {}, {}, {}, {}, {}
@@ -273,7 +275,7 @@ def tile_bcnnresnet_kernel(tc, feat, W, b, out):
                 return
             s = 2 * k
             e = slice(s % CH, s % CH + 2)
-            Wp = wp_tiles[s // CH]
+            Wp = wp_tiles.get(s // CH)
             if s >= HM:
                 nc.vector.memset(Wp[:, :, e, HD - OCT:HD], 0.0)
                 return
@@ -423,8 +425,12 @@ def tile_bcnnresnet_kernel(tc, feat, W, b, out):
             old2 = plan.get(s - 2, [])
             if s % 2 == 0 and s // 2 + 2 < K16:
                 load_fm(s // 2 + 2)
-            if s % CH == 2:
-                load_w2(s // CH + 2)
+            if s % CH == 0:
+                load_w2(s // CH + 4)
+            for w, h in old2:
+                stage_mx1(w, h)
+            for w, h in old:
+                stage_wq(h, w)
             if s % 2 == 1:
                 stage_tab_s(s // 2 + 1)
             stage_sqrt(s + 3, 0)
@@ -449,14 +455,10 @@ def tile_bcnnresnet_kernel(tc, feat, W, b, out):
             stage_e(s, 2)
             stage_sign(s + 2, 2)
             stage_e(s, 3)
-            for w, h in old2:
-                stage_mx1(w, h)
             stage_t(s + 1, 2)
             stage_sign(s + 2, 3)
             stage_sign2(s + 2)
             stage_q(s)
-            for w, h in old:
-                stage_wq(h, w)
             if s % 2 == 1:
                 stage_w2mix((s + 3) // 2)
             stage_q2(s, 0)

@@ -42,7 +42,6 @@ def tile_bcnnresnet_kernel(tc, feat, W, b, out):
         wcpool = ctx.enter_context(tc.tile_pool(name="wcpool", bufs=2))
         wc2pool = ctx.enter_context(tc.tile_pool(name="wc2pool", bufs=2))
         tabp = ctx.enter_context(tc.tile_pool(name="tabp", bufs=2))
-        fmp = ctx.enter_context(tc.tile_pool(name="fmp", bufs=3))
         accp = ctx.enter_context(tc.psum_pool(name="accp", bufs=1))
         tps = ctx.enter_context(tc.psum_pool(name="tps", bufs=5))
         wps = ctx.enter_context(tc.psum_pool(name="wps", bufs=1))
@@ -56,11 +55,13 @@ def tile_bcnnresnet_kernel(tc, feat, W, b, out):
         A = const.tile([P, NG, D], BF16, name="A")
         SI = const.tile([P, NG, HM], F32, name="SI")
         SIp = const.tile([P, HM, NG, 2], BF16, name="SIp")
-        alpha = const.tile([P, NG * NM], F32, name="alpha")
+        alpha = const.tile([P, NG, NM], F32, name="alpha")
         bb = const.tile([P, C], BF16, name="bb")
         ident_bf = const.tile([P, P], BF16, name="ident_bf")
         ident_f = const.tile([P, P], F32, name="ident_f")
         T16 = const.tile([P, B, 2], BF16, name="T16")
+        Fn = const.tile([P, B // P, D], BF16, name="Fn")
+        Fm = const.tile([P, B // P, HD], BF16, name="Fm")
         Wa = const.tile([P, C, HD], BF16, name="Wa")
         Wb = const.tile([P, C, D], BF16, name="Wb")
         mask_a = const.tile([P, P], BF16, name="mask_a")
@@ -74,19 +75,7 @@ def tile_bcnnresnet_kernel(tc, feat, W, b, out):
             for n in ("Ssum", "nz", "sq", "nq", "nqe", "n2", "nrm", "nrc", "rn0", "r2", "hh", "hn", "rn", "rn2", "beta")
         ]
 
-        fm_tiles, wr_tiles, wp_tiles = {}, {}, {}
-
-        def load_fm(k):
-            if k > HD // OCT:
-                return
-            Fm = fmp.tile([P, B // P, HD], BF16, name="Fm")
-            lo = OCT * k
-            if k > 0:
-                hi = min(HD, lo + OCT * (k % 2))
-                nc.sync.dma_start(out=Fm[:, :, 0:hi], in_=feat_n[:, :, HD:HD + hi])
-            if lo < HD:
-                nc.sync.dma_start(out=Fm[:, :, lo:HD], in_=feat_n[:, :, lo:HD])
-            fm_tiles[k] = Fm
+        wr_tiles, wp_tiles = {}, {}
 
         def load_w2(ch):
             s0 = ch * CH
@@ -111,86 +100,22 @@ def tile_bcnnresnet_kernel(tc, feat, W, b, out):
                 cs = slice(q * 32, q * 32 + 32)
                 nc.sync.dma_start(out=dst[:, cs, i0:i0 + HD], in_=W_n[j0:j0 + HD, cs, i0:i0 + HD])
 
-        with tc.tile_pool(name="pro", bufs=1) as pro:
-            F = pro.tile([P, NG, D], BF16, name="F")
-            Fs = pro.tile([P, NG, D], BF16, name="Fs")
-            nonzero = pro.tile([P, NG, D], BF16, name="nonzero")
-            AI = pro.tile([P, NG * NM], F32, name="AI")
-            SH = D - PACK + 1
-            queues = [nc.sync, nc.scalar, nc.sync, nc.scalar]
-            for t in range(PACK):
-                queues[t].dma_start(out=F[t:P:PACK, :, :], in_=feat_v)
-            for t in range(PACK):
-                queues[t].dma_start(out=Fs[t:P:PACK, :, 0:SH], in_=feat_v[:, :, t:t + SH])
-            nc.gpsimd.dma_start(out=bb[:], in_=b.partition_broadcast(P))
-            load_fm(HD // OCT)
-            load_fm(0)
-            load_w2(0)
-            load_fm(1)
-            load_w2(1)
-            load_wn(Wb, HD, 0)
-            load_w2(2)
-            load_w2(3)
-            load_wn(Wb, HD, HD)
-            load_wn(Wa, 0, 0)
-            make_identity(nc, ident_bf[:])
-            make_identity(nc, ident_f[:])
-            nc.gpsimd.tensor_copy(out=mask_a[:], in_=ident_bf[:])
-            nc.gpsimd.memset(mask_b[:], 0.0)
-            FI = Fs[:, :, 0:SH:PACK]
-            HG = NG // 2
-            for h in range(2):
-                gs = slice(h * HG, (h + 1) * HG)
-                for g in range(h * HG, (h + 1) * HG):
-                    nc.scalar.activation(out=A[:, g, :], in_=F[:, g, :], func=ACT.Abs, accum_out=Ssum[:, g:g + 1])
-                nc.vector.tensor_scalar(out=nonzero[:, gs, :], in0=F[:, gs, :], scalar1=0.0, scalar2=None, op0=ALU.not_equal)
-                nc.vector.tensor_reduce(out=nz[:, gs], in_=nonzero[:, gs, :], axis=AX.X, op=ALU.add)
-            for h in range(2):
-                gs = slice(h * HG, (h + 1) * HG)
-                cs = slice(h * HG * NM, (h + 1) * HG * NM)
-                nc.scalar.activation(out=AI[:, cs].rearrange("q (g m) -> q g m", m=NM), in_=FI[:, gs, :], func=ACT.Abs)
-                nc.scalar.activation(out=SI[:, gs, :], in_=FI[:, gs, 0:HM], func=ACT.Sign)
-            nc.scalar.activation(out=SIp[:], in_=FI[:, :, HM:NM].rearrange("q g m -> q m g").unsqueeze(3).to_broadcast([P, HM, NG, 2]), func=ACT.Sign)
-            for h in range(2):
-                gs = slice(h * HG, (h + 1) * HG)
-                cs = slice(h * HG * NM, (h + 1) * HG * NM)
-                nc.vector.tensor_tensor(out=sq[:, gs], in0=Ssum[:, gs], in1=Ssum[:, gs], op=ALU.mult)
-                nc.vector.tensor_tensor(out=nq[:, gs], in0=nz[:, gs], in1=nz[:, gs], op=ALU.mult)
-                nc.vector.tensor_scalar(out=nqe[:, gs], in0=nq[:, gs], scalar1=EPS_SQRT, scalar2=None, op0=ALU.mult)
-                nc.vector.tensor_tensor(out=n2[:, gs], in0=sq[:, gs], in1=nqe[:, gs], op=ALU.add)
-                nc.scalar.activation(out=nrm[:, gs], in_=n2[:, gs], func=ACT.Sqrt)
-                nc.vector.tensor_scalar(out=nrc[:, gs], in0=nrm[:, gs], scalar1=EPS_NORM, scalar2=None, op0=ALU.max)
-                nc.vector.reciprocal(out=rn0[:, gs], in_=nrc[:, gs])
-                nc.vector.tensor_tensor(out=r2[:, gs], in0=rn0[:, gs], in1=rn0[:, gs], op=ALU.mult)
-                nc.vector.tensor_tensor(out=hh[:, gs], in0=r2[:, gs], in1=n2[:, gs], op=ALU.mult)
-                nc.vector.tensor_scalar(out=hn[:, gs], in0=hh[:, gs], scalar1=-0.5, scalar2=1.5, op0=ALU.mult, op1=ALU.add)
-                nc.vector.tensor_tensor(out=rn[:, gs], in0=rn0[:, gs], in1=hn[:, gs], op=ALU.mult)
-                nc.vector.tensor_tensor(out=rn2[:, gs], in0=rn[:, gs], in1=rn[:, gs], op=ALU.mult)
-                nc.vector.tensor_scalar(out=beta[:, gs], in0=rn2[:, gs], scalar1=EPS_SQRT, scalar2=None, op0=ALU.mult)
-                nc.vector.tensor_tensor(
-                    out=alpha[:, cs].rearrange("q (g m) -> q g m", m=NM),
-                    in0=AI[:, cs].rearrange("q (g m) -> q g m", m=NM),
-                    in1=rn2[:, gs].unsqueeze(2).to_broadcast([P, HG, NM]),
-                    op=ALU.mult,
-                )
-
-        xrpool = ctx.enter_context(tc.tile_pool(name="xrpool", bufs=4))
-        xmpool = ctx.enter_context(tc.tile_pool(name="xmpool", bufs=10))
         acc = accp.tile([P, B], F32, name="acc")
 
         z_tiles, t_tiles, g_tiles, xa_tiles, xb_tiles = {}, {}, {}, {}, {}
         wt_tiles, wg_tiles, wq_tiles, tt_tiles, tabs = {}, {}, {}, {}, {HD // OCT: T16}
         mix_tiles, mask_k = {}, [0]
-        passes = []
+        passes, late = [], {}
         N_PASS = 4 * HM + 2 * (NS - HM)
 
         def stage_tab_t(k):
-            if k not in fm_tiles:
-                return
-            Fm = fm_tiles.pop(k)
+            if 0 < k < HD // OCT:
+                cs = slice(OCT * (k - 1), OCT * k)
+                nc.gpsimd.tensor_copy(out=Fm[:, :, cs], in_=Fn[:, :, HD + OCT * (k - 1):HD + OCT * k])
             ps = tps.tile([P, B], BF16, name="pst", tag="t")
             for tl in range(B // P):
-                nc.tensor.transpose(out=ps[:, tl * P:(tl + 1) * P], in_=Fm[:, tl, :], identity=ident_bf[:])
+                src = Fn[:, tl, HD:D] if k == HD // OCT else Fm[:, tl, :]
+                nc.tensor.transpose(out=ps[:, tl * P:(tl + 1) * P], in_=src, identity=ident_bf[:])
             tt_tiles[k] = ps
 
         def stage_tab_s(k):
@@ -198,7 +123,7 @@ def tile_bcnnresnet_kernel(tc, feat, W, b, out):
                 return
             if k not in tabs:
                 tabs[k] = tabp.tile([P, B, 2], BF16, name="T")
-            nc.scalar.activation(out=tabs[k][:], in_=tt_tiles.pop(k)[:].unsqueeze(2).to_broadcast([P, B, 2]), func=ACT.Sign)
+            nc.scalar.copy(out=tabs[k][:], in_=tt_tiles.pop(k)[:].unsqueeze(2).to_broadcast([P, B, 2]))
 
         def stage_sqrt(s, q):
             if s >= NS:
@@ -209,11 +134,10 @@ def tile_bcnnresnet_kernel(tc, feat, W, b, out):
             lo = OCT * (s // 2)
             for g in range(4 * q, 4 * q + 4):
                 if s < HM:
-                    col = g * NM + s
-                    nc.scalar.activation(out=Z[:, g, lo:D], in_=A[:, g, lo:D], func=ACT.Sqrt, bias=beta[:, g:g + 1], scale=alpha[:, col:col + 1])
+                    nc.scalar.activation(out=Z[:, g, lo:D], in_=A[:, g, lo:D], func=ACT.Sqrt, bias=beta[:, g:g + 1], scale=alpha[:, g, s:s + 1])
                 if s >= 2:
-                    col = g * NM + HM - 2 + s
-                    nc.scalar.activation(out=Z[:, g, 0:lo], in_=A[:, g, HD:HD + lo], func=ACT.Sqrt, bias=beta[:, g:g + 1], scale=alpha[:, col:col + 1])
+                    m = HM - 2 + s
+                    nc.scalar.activation(out=Z[:, g, 0:lo], in_=A[:, g, HD:HD + lo], func=ACT.Sqrt, bias=beta[:, g:g + 1], scale=alpha[:, g, m:m + 1])
 
         def stage_sign(s, q):
             if s >= HM:
@@ -243,7 +167,7 @@ def tile_bcnnresnet_kernel(tc, feat, W, b, out):
         def stage_e(s, j):
             if s >= HM and j >= 2:
                 return
-            if j == 0:
+            if s not in g_tiles:
                 g_tiles[s] = gpool.tile([P, 2 * NG * P], BF16, name="G", align_bytes=64)
             T = tabs[s // 2] if j < 2 else T16
             h = j % 2
@@ -264,7 +188,7 @@ def tile_bcnnresnet_kernel(tc, feat, W, b, out):
         def stage_q2(s, h):
             if s >= HM and h == 1:
                 return
-            pool = xrpool if h == 1 else xmpool
+            pool = late[h]
             Xc = pool.tile([P, B], U32, name="Yc", align_bytes=64)
             Xs = pool.tile([P, B], U8, name="Ys", align_bytes=64)
             nc.vector.quantize_mx(out=Xc[:].bitcast(FP8X4), scales=Xs[:], in_=g_tiles[s][:, h * PACK * B:(h + 1) * PACK * B])
@@ -397,25 +321,122 @@ def tile_bcnnresnet_kernel(tc, feat, W, b, out):
                         plan[s].append((nxt, h))
                         nxt += 1
 
-        ctx.enter_context(tc.manual_schedule())
         K16 = HD // OCT
-        for q in range(4):
-            stage_sqrt(0, q)
-        stage_tab_t(K16)
-        stage_tab_t(0)
-        stage_tab_s(K16)
-        stage_tab_s(0)
-        for q in range(4):
-            stage_sqrt(1, q)
+        ctx.enter_context(tc.manual_schedule())
+        with tc.tile_pool(name="pro", bufs=1) as pro:
+            F = pro.tile([P, NG, D], BF16, name="F")
+            Fs = pro.tile([P, NG, D], BF16, name="Fs")
+            nonzero = pro.tile([P, NG, D], BF16, name="nonzero")
+            AI = pro.tile([P, NG, NM], F32, name="AI")
+            FIn = pro.tile([P, NG, NM], BF16, name="FIn")
+            Fraw = pro.tile([P, B // P, D], BF16, name="Fraw")
+            one = pro.tile([P, 1], F32, name="one")
+            SH = D - PACK + 1
+            HG = NG // 2
+            queues = [nc.sync, nc.scalar, nc.sync, nc.scalar]
+            for h in range(2):
+                for t in range(PACK):
+                    queues[t].dma_start(out=F[t:P:PACK, h * HG:(h + 1) * HG, :], in_=feat_v[:, h * HG:(h + 1) * HG, :])
+            nc.sync.dma_start(out=Fraw[:], in_=feat_n)
+            for t in range(PACK):
+                queues[t].dma_start(out=Fs[t:P:PACK, :, 0:SH], in_=feat_v[:, :, t:t + SH])
+            nc.gpsimd.dma_start(out=bb[:], in_=b.partition_broadcast(P))
+            load_w2(0)
+            load_w2(1)
+            load_wn(Wb, HD, 0)
+            load_w2(2)
+            load_w2(3)
+            make_identity(nc, ident_bf[:])
+            make_identity(nc, ident_f[:])
+            nc.gpsimd.tensor_copy(out=mask_a[:], in_=ident_bf[:])
+            nc.gpsimd.memset(mask_b[:], 0.0)
+            nc.vector.memset(one[:], 1.0)
+            nc.scalar.activation(out=one[:], in_=one[:], func=ACT.Sqrt)
+            FI = Fs[:, :, 0:SH:PACK]
+
+            def head_count(h):
+                gs = slice(h * HG, (h + 1) * HG)
+                nc.vector.tensor_scalar(out=nonzero[:, gs, :], in0=F[:, gs, :], scalar1=0.0, scalar2=None, op0=ALU.not_equal)
+                nc.vector.tensor_reduce(out=nz[:, gs], in_=nonzero[:, gs, :], axis=AX.X, op=ALU.add)
+
+            def head_abs_i(h):
+                gs = slice(h * HG, (h + 1) * HG)
+                nc.vector.tensor_scalar(out=FIn[:, gs, :], in0=FI[:, gs, :], scalar1=-1.0, scalar2=None, op0=ALU.mult)
+                nc.vector.tensor_tensor(out=AI[:, gs, :], in0=FI[:, gs, :], in1=FIn[:, gs, :], op=ALU.max)
+
+            def head_norm(h):
+                gs = slice(h * HG, (h + 1) * HG)
+                nc.vector.tensor_tensor(out=sq[:, gs], in0=Ssum[:, gs], in1=Ssum[:, gs], op=ALU.mult)
+                nc.vector.tensor_tensor(out=nq[:, gs], in0=nz[:, gs], in1=nz[:, gs], op=ALU.mult)
+                nc.vector.tensor_scalar(out=nqe[:, gs], in0=nq[:, gs], scalar1=EPS_SQRT, scalar2=None, op0=ALU.mult)
+                nc.vector.tensor_tensor(out=n2[:, gs], in0=sq[:, gs], in1=nqe[:, gs], op=ALU.add)
+                nc.scalar.activation(out=nrm[:, gs], in_=n2[:, gs], func=ACT.Sqrt)
+
+            def head_scale(h):
+                gs = slice(h * HG, (h + 1) * HG)
+                nc.vector.tensor_scalar(out=nrc[:, gs], in0=nrm[:, gs], scalar1=EPS_NORM, scalar2=None, op0=ALU.max)
+                nc.vector.reciprocal(out=rn0[:, gs], in_=nrc[:, gs])
+                nc.vector.tensor_tensor(out=r2[:, gs], in0=rn0[:, gs], in1=rn0[:, gs], op=ALU.mult)
+                nc.vector.tensor_tensor(out=hh[:, gs], in0=r2[:, gs], in1=n2[:, gs], op=ALU.mult)
+                nc.vector.tensor_scalar(out=hn[:, gs], in0=hh[:, gs], scalar1=-0.5, scalar2=1.5, op0=ALU.mult, op1=ALU.add)
+                nc.vector.tensor_tensor(out=rn[:, gs], in0=rn0[:, gs], in1=hn[:, gs], op=ALU.mult)
+                nc.vector.tensor_tensor(out=rn2[:, gs], in0=rn[:, gs], in1=rn[:, gs], op=ALU.mult)
+                nc.vector.tensor_scalar(out=beta[:, gs], in0=rn2[:, gs], scalar1=EPS_SQRT, scalar2=None, op0=ALU.mult)
+                nc.vector.tensor_tensor(
+                    out=alpha[:, gs, :], in0=AI[:, gs, :], in1=rn2[:, gs].unsqueeze(2).to_broadcast([P, HG, NM]), op=ALU.mult
+                )
+
+            def head_abs(g0, g1):
+                for g in range(g0, g1):
+                    nc.scalar.activation(out=A[:, g, :], in_=F[:, g, :], func=ACT.Abs, accum_out=Ssum[:, g:g + 1])
+
+            head_abs(0, 8)
+            head_count(0)
+            nc.scalar.activation(out=Fn[:], in_=Fraw[:], func=ACT.Sign)
+            nc.gpsimd.tensor_copy(out=Fm[:], in_=Fn[:, :, 0:HD])
+            head_abs(8, 11)
+            head_norm(0)
+            stage_tab_t(0)
+            stage_tab_t(K16)
+            head_abs_i(0)
+            head_abs(11, 16)
+            head_scale(0)
+            stage_tab_s(0)
+            nc.scalar.activation(out=SI[:], in_=FI[:, :, 0:HM], func=ACT.Sign)
+            stage_sqrt(0, 0)
+            head_count(1)
+            head_norm(1)
+            stage_sqrt(0, 1)
+            head_abs_i(1)
+            head_scale(1)
+            stage_sqrt(0, 2)
+            stage_tab_s(K16)
+            stage_sqrt(0, 3)
+            stage_sign(0, 0)
+            stage_sign(0, 1)
+            stage_t(0, 0)
+            stage_t(0, 2)
+            nc.scalar.activation(out=SIp[:], in_=FI[:, :, HM:NM].rearrange("q g m -> q m g").unsqueeze(3).to_broadcast([P, HM, NG, 2]), func=ACT.Sign)
+
+        late[1] = ctx.enter_context(tc.tile_pool(name="xrpool", bufs=4))
+        late[0] = ctx.enter_context(tc.tile_pool(name="xmpool", bufs=10))
+        stage_sign(0, 2)
         stage_w2mix(0)
+        stage_sign(0, 3)
+        stage_e(0, 0)
+        stage_t(0, 1)
+        stage_t(0, 3)
         stage_w2mix(1)
+        stage_e(0, 2)
         stage_w2t(0)
+        stage_sqrt(1, 0)
+        stage_sqrt(1, 1)
         stage_w2c(0)
         stage_w2t(1)
-        for q in range(4):
-            stage_sign(0, q)
-        for j in range(4):
-            stage_t(0, j)
+        stage_e(0, 1)
+        stage_e(0, 3)
+        stage_sqrt(1, 2)
+        stage_sqrt(1, 3)
         for q in range(4):
             stage_sqrt(2, q)
         for q in range(4):
@@ -423,38 +444,43 @@ def tile_bcnnresnet_kernel(tc, feat, W, b, out):
         for s in range(NS):
             old = plan.get(s - 1, [])
             old2 = plan.get(s - 2, [])
-            if s % 2 == 0 and s // 2 + 2 < K16:
-                load_fm(s // 2 + 2)
             if s % CH == 0:
                 load_w2(s // CH + 4)
+            if s == 0:
+                load_wn(Wb, HD, HD)
+            if s == 2:
+                load_wn(Wa, 0, 0)
             for w, h in old2:
                 stage_mx1(w, h)
-            for w, h in old:
-                stage_wq(h, w)
-            if s % 2 == 1:
-                stage_tab_s(s // 2 + 1)
-            stage_sqrt(s + 3, 0)
-            stage_w2c(s + 1)
-            stage_sqrt(s + 3, 1)
-            for w, h in plan[s]:
-                stage_w1c(w, h)
             stage_mx2(s - 1)
             if s % 2 == 0 and s // 2 + 1 < K16:
                 stage_tab_t(s // 2 + 1)
-            stage_e(s, 0)
+            stage_w2c(s + 1)
+            stage_sqrt(s + 3, 0)
+            stage_sqrt(s + 3, 1)
+            stage_tab_s(s // 2 + 1)
+            if s > 0:
+                stage_e(s, 0)
             stage_t(s + 1, 0)
             stage_sign(s + 2, 0)
             stage_wq(2, s)
-            stage_e(s, 1)
+            if s > 0:
+                stage_e(s, 1)
             stage_t(s + 1, 1)
             stage_idle(s - 1, 2)
             stage_w2t(s + 2)
+            stage_sign(s + 2, 1)
+            for w, h in old:
+                stage_wq(h, w)
+            for w, h in plan[s]:
+                stage_w1c(w, h)
             stage_sqrt(s + 3, 2)
             stage_sqrt(s + 3, 3)
-            stage_sign(s + 2, 1)
-            stage_e(s, 2)
+            if s > 0:
+                stage_e(s, 2)
             stage_sign(s + 2, 2)
-            stage_e(s, 3)
+            if s > 0:
+                stage_e(s, 3)
             stage_t(s + 1, 2)
             stage_sign(s + 2, 3)
             stage_sign2(s + 2)

@@ -43,8 +43,9 @@ def tile_bcnnresnet_kernel(tc, feat, W, b, out):
         wc2pool = ctx.enter_context(tc.tile_pool(name="wc2pool", bufs=2))
         tabp = ctx.enter_context(tc.tile_pool(name="tabp", bufs=2))
         accp = ctx.enter_context(tc.psum_pool(name="accp", bufs=1))
-        tps = ctx.enter_context(tc.psum_pool(name="tps", bufs=5))
+        tps = ctx.enter_context(tc.psum_pool(name="tps", bufs=4))
         wps = ctx.enter_context(tc.psum_pool(name="wps", bufs=1))
+        aux = ctx.enter_context(tc.psum_pool(name="aux", bufs=1))
         dps = ctx.enter_context(tc.psum_pool(name="dps", bufs=1))
 
         feat_v = feat.rearrange("(g nl) j -> nl g j", nl=NL)
@@ -112,7 +113,7 @@ def tile_bcnnresnet_kernel(tc, feat, W, b, out):
             if 0 < k < HD // OCT:
                 cs = slice(OCT * (k - 1), OCT * k)
                 nc.gpsimd.tensor_copy(out=Fm[:, :, cs], in_=Fn[:, :, HD + OCT * (k - 1):HD + OCT * k])
-            ps = tps.tile([P, B], BF16, name="pst", tag="t")
+            ps = aux.tile([P, B], BF16, name="pst", tag="x")
             for tl in range(B // P):
                 src = Fn[:, tl, HD:D] if k == HD // OCT else Fm[:, tl, :]
                 nc.tensor.transpose(out=ps[:, tl * P:(tl + 1) * P], in_=src, identity=ident_bf[:])
@@ -235,7 +236,7 @@ def tile_bcnnresnet_kernel(tc, feat, W, b, out):
             todo = [s for s, h in todo if mixes(s, h)]
             if not todo:
                 return
-            ps = dps.tile([P, 2, 4 * P], BF16, name="mix", tag="d")
+            ps = aux.tile([P, 2, 4 * P], BF16, name="mix", tag="x")
             for n, s in enumerate(todo):
                 k = s // 2
                 while mask_k[0] < k:
@@ -258,7 +259,7 @@ def tile_bcnnresnet_kernel(tc, feat, W, b, out):
             dst = Wg[:].bitcast(F32).rearrange("p (c w) -> p c w", w=2)
             Va, Vb = Wa[:].bitcast(F32), Wb[:].bitcast(F32)
             if h == 1:
-                nc.scalar.copy(out=dst, in_=Vb[:, :, 2 * s:2 * s + 2])
+                nc.vector.tensor_copy(out=dst, in_=Vb[:, :, 2 * s:2 * s + 2])
                 return
             b0 = (HD - OCT) // 2 + 2 * s
             lo = OCT * (s // 2)
@@ -364,12 +365,15 @@ def tile_bcnnresnet_kernel(tc, feat, W, b, out):
                 nc.vector.tensor_scalar(out=FIn[:, gs, :], in0=FI[:, gs, :], scalar1=-1.0, scalar2=None, op0=ALU.mult)
                 nc.vector.tensor_tensor(out=AI[:, gs, :], in0=FI[:, gs, :], in1=FIn[:, gs, :], op=ALU.max)
 
-            def head_norm(h):
+            def head_norm_v(h):
                 gs = slice(h * HG, (h + 1) * HG)
                 nc.vector.tensor_tensor(out=sq[:, gs], in0=Ssum[:, gs], in1=Ssum[:, gs], op=ALU.mult)
                 nc.vector.tensor_tensor(out=nq[:, gs], in0=nz[:, gs], in1=nz[:, gs], op=ALU.mult)
                 nc.vector.tensor_scalar(out=nqe[:, gs], in0=nq[:, gs], scalar1=EPS_SQRT, scalar2=None, op0=ALU.mult)
                 nc.vector.tensor_tensor(out=n2[:, gs], in0=sq[:, gs], in1=nqe[:, gs], op=ALU.add)
+
+            def head_norm_s(h):
+                gs = slice(h * HG, (h + 1) * HG)
                 nc.scalar.activation(out=nrm[:, gs], in_=n2[:, gs], func=ACT.Sqrt)
 
             def head_scale(h):
@@ -392,55 +396,48 @@ def tile_bcnnresnet_kernel(tc, feat, W, b, out):
 
             head_abs(0, 8)
             head_count(0)
+            head_norm_v(0)
             nc.scalar.activation(out=Fn[:], in_=Fraw[:], func=ACT.Sign)
             nc.gpsimd.tensor_copy(out=Fm[:], in_=Fn[:, :, 0:HD])
-            head_abs(8, 11)
-            head_norm(0)
+            head_norm_s(0)
             stage_tab_t(0)
-            stage_tab_t(K16)
             head_abs_i(0)
-            head_abs(11, 16)
+            head_abs(8, 16)
             head_scale(0)
             stage_tab_s(0)
+            stage_tab_t(K16)
             nc.scalar.activation(out=SI[:], in_=FI[:, :, 0:HM], func=ACT.Sign)
-            stage_sqrt(0, 0)
             head_count(1)
-            head_norm(1)
+            head_norm_v(1)
+            stage_sqrt(0, 0)
             stage_sqrt(0, 1)
+            head_norm_s(1)
+            stage_tab_s(K16)
+            stage_sqrt(1, 0)
             head_abs_i(1)
             head_scale(1)
             stage_sqrt(0, 2)
-            stage_tab_s(K16)
             stage_sqrt(0, 3)
             stage_sign(0, 0)
             stage_sign(0, 1)
-            stage_t(0, 0)
             stage_t(0, 2)
+            stage_t(0, 0)
             nc.scalar.activation(out=SIp[:], in_=FI[:, :, HM:NM].rearrange("q g m -> q m g").unsqueeze(3).to_broadcast([P, HM, NG, 2]), func=ACT.Sign)
 
         late[1] = ctx.enter_context(tc.tile_pool(name="xrpool", bufs=4))
         late[0] = ctx.enter_context(tc.tile_pool(name="xmpool", bufs=10))
-        stage_sign(0, 2)
         stage_w2mix(0)
+        stage_sign(0, 2)
         stage_sign(0, 3)
-        stage_e(0, 0)
-        stage_t(0, 1)
         stage_t(0, 3)
-        stage_w2mix(1)
-        stage_e(0, 2)
+        stage_t(0, 1)
         stage_w2t(0)
-        stage_sqrt(1, 0)
         stage_sqrt(1, 1)
         stage_w2c(0)
         stage_w2t(1)
-        stage_e(0, 1)
-        stage_e(0, 3)
         stage_sqrt(1, 2)
         stage_sqrt(1, 3)
-        for q in range(4):
-            stage_sqrt(2, q)
-        for q in range(4):
-            stage_sign(1, q)
+        stage_w2mix(1)
         for s in range(NS):
             old = plan.get(s - 1, [])
             old2 = plan.get(s - 2, [])
@@ -453,45 +450,45 @@ def tile_bcnnresnet_kernel(tc, feat, W, b, out):
             for w, h in old2:
                 stage_mx1(w, h)
             stage_mx2(s - 1)
-            if s % 2 == 0 and s // 2 + 1 < K16:
-                stage_tab_t(s // 2 + 1)
-            stage_w2c(s + 1)
-            stage_sqrt(s + 3, 0)
-            stage_sqrt(s + 3, 1)
-            stage_tab_s(s // 2 + 1)
-            if s > 0:
-                stage_e(s, 0)
-            stage_t(s + 1, 0)
-            stage_sign(s + 2, 0)
-            stage_wq(2, s)
-            if s > 0:
-                stage_e(s, 1)
-            stage_t(s + 1, 1)
-            stage_idle(s - 1, 2)
-            stage_w2t(s + 2)
-            stage_sign(s + 2, 1)
+            stage_e(s, 2)
+            stage_sign(s + 1, 0)
             for w, h in old:
                 stage_wq(h, w)
+            stage_w2c(s + 1)
             for w, h in plan[s]:
-                stage_w1c(w, h)
-            stage_sqrt(s + 3, 2)
-            stage_sqrt(s + 3, 3)
-            if s > 0:
-                stage_e(s, 2)
-            stage_sign(s + 2, 2)
-            if s > 0:
-                stage_e(s, 3)
+                if h == 0:
+                    stage_w1c(w, h)
+            stage_sqrt(s + 2, 0)
+            stage_sqrt(s + 2, 1)
+            if s % 2 == 0 and s // 2 + 1 < K16:
+                stage_tab_t(s // 2 + 1)
+            stage_tab_s(s // 2 + 1)
+            stage_e(s, 3)
+            stage_sign(s + 1, 1)
             stage_t(s + 1, 2)
-            stage_sign(s + 2, 3)
-            stage_sign2(s + 2)
+            stage_idle(s - 1, 2)
+            stage_wq(2, s)
+            stage_e(s, 0)
+            stage_sign(s + 1, 2)
+            stage_w2t(s + 2)
+            for w, h in plan[s]:
+                if h == 1:
+                    stage_w1c(w, h)
+            stage_sqrt(s + 2, 2)
+            stage_sqrt(s + 2, 3)
+            stage_e(s, 1)
+            stage_sign(s + 1, 3)
+            stage_t(s + 1, 3)
+            stage_sign2(s + 1)
+            stage_mix(plan.get(s + 1, []))
+            stage_idle(s - 1, 2)
+            stage_t(s + 1, 0)
             stage_q(s)
+            stage_t(s + 1, 1)
             if s % 2 == 1:
                 stage_w2mix((s + 3) // 2)
             stage_q2(s, 0)
             stage_q2(s, 1)
-            stage_t(s + 1, 3)
-            stage_idle(s - 1, 2)
-            stage_mix(plan.get(s + 1, []))
         stage_mx2(NS - 1)
         for w, h in plan[NS - 2]:
             stage_mx1(w, h)

@@ -25,7 +25,7 @@ NS = HM + 2
 CH = 2
 EPS_SQRT = 1e-10
 EPS_NORM = 1e-12
-START_R, START_M = 2, 8
+START_R, START_M = 4, 9
 FLOPS = 2 * B * D * D * C
 
 
@@ -36,10 +36,10 @@ def tile_bcnnresnet_kernel(tc, feat, W, b, out):
         zpool = ctx.enter_context(tc.tile_pool(name="zpool", bufs=3))
         gpool = ctx.enter_context(tc.tile_pool(name="gpool", bufs=1))
         xapool = ctx.enter_context(tc.tile_pool(name="xapool", bufs=2))
-        wrpool = ctx.enter_context(tc.tile_pool(name="wrpool", bufs=4))
+        wrpool = ctx.enter_context(tc.tile_pool(name="wrpool", bufs=3))
         wgpool = ctx.enter_context(tc.tile_pool(name="wgpool", bufs=2))
         wg2pool = ctx.enter_context(tc.tile_pool(name="wg2pool", bufs=2))
-        wcpool = ctx.enter_context(tc.tile_pool(name="wcpool", bufs=2))
+        wcpool = ctx.enter_context(tc.tile_pool(name="wcpool", bufs=3))
         wc2pool = ctx.enter_context(tc.tile_pool(name="wc2pool", bufs=2))
         tabp = ctx.enter_context(tc.tile_pool(name="tabp", bufs=2))
         accp = ctx.enter_context(tc.psum_pool(name="accp", bufs=1))
@@ -68,13 +68,7 @@ def tile_bcnnresnet_kernel(tc, feat, W, b, out):
         mask_a = const.tile([P, P], BF16, name="mask_a")
         mask_b = const.tile([P, P], BF16, name="mask_b")
 
-        def small(name):
-            return const.tile([P, NG], F32, name=name)
-
-        Ssum, nz, sq, nq, nqe, n2, nrm, nrc, rn0, r2, hh, hn, rn, rn2, beta = [
-            small(n)
-            for n in ("Ssum", "nz", "sq", "nq", "nqe", "n2", "nrm", "nrc", "rn0", "r2", "hh", "hn", "rn", "rn2", "beta")
-        ]
+        beta = const.tile([P, NG], F32, name="beta")
 
         wr_tiles, wp_tiles = {}, {}
 
@@ -96,10 +90,9 @@ def tile_bcnnresnet_kernel(tc, feat, W, b, out):
                     nc.sync.dma_start(out=Wp[t:P:PACK, :, e, :], in_=W_v[t, HM - 2 + s0 + e, :, :, HD:D])
             wp_tiles[ch] = Wp
 
-        def load_wn(dst, j0, i0):
-            for q in range(4):
-                cs = slice(q * 32, q * 32 + 32)
-                nc.sync.dma_start(out=dst[:, cs, i0:i0 + HD], in_=W_n[j0:j0 + HD, cs, i0:i0 + HD])
+        def load_wn(dst, j0, i0, q):
+            cs = slice(q * NL, q * NL + NL)
+            nc.sync.dma_start(out=dst[:, cs, i0:i0 + HD], in_=W_n[j0:j0 + HD, cs, i0:i0 + HD])
 
         acc = accp.tile([P, B], F32, name="acc")
 
@@ -202,13 +195,13 @@ def tile_bcnnresnet_kernel(tc, feat, W, b, out):
             e = slice(s % CH, s % CH + 2)
             Wp = wp_tiles.get(s // CH)
             if s >= HM:
-                nc.vector.memset(Wp[:, :, e, HD - OCT:HD], 0.0)
+                nc.gpsimd.memset(Wp[:, :, e, HD - OCT:HD], 0.0)
                 return
             Wr = wr_tiles[s // CH]
             lo = OCT * k
-            nc.vector.memset(Wr[:, :, e, max(0, lo - OCT):lo + OCT], 0.0)
+            nc.gpsimd.memset(Wr[:, :, e, max(0, lo - OCT):lo + OCT], 0.0)
             if k >= 2:
-                nc.vector.tensor_copy(out=Wr[:, :, e, 0:lo - OCT], in_=Wp[:, :, e, 0:lo - OCT])
+                nc.scalar.copy(out=Wr[:, :, e, 0:lo - OCT], in_=Wp[:, :, e, 0:lo - OCT])
 
         def stage_w2t(s):
             if s >= NS:
@@ -259,7 +252,7 @@ def tile_bcnnresnet_kernel(tc, feat, W, b, out):
             dst = Wg[:].bitcast(F32).rearrange("p (c w) -> p c w", w=2)
             Va, Vb = Wa[:].bitcast(F32), Wb[:].bitcast(F32)
             if h == 1:
-                nc.vector.tensor_copy(out=dst, in_=Vb[:, :, 2 * s:2 * s + 2])
+                nc.scalar.copy(out=dst, in_=Vb[:, :, 2 * s:2 * s + 2])
                 return
             b0 = (HD - OCT) // 2 + 2 * s
             lo = OCT * (s // 2)
@@ -332,21 +325,30 @@ def tile_bcnnresnet_kernel(tc, feat, W, b, out):
             FIn = pro.tile([P, NG, NM], BF16, name="FIn")
             Fraw = pro.tile([P, B // P, D], BF16, name="Fraw")
             one = pro.tile([P, 1], F32, name="one")
+
+            def small(name):
+                return pro.tile([P, NG], F32, name=name)
+
+            Ssum, nz, sq, nq, nqe, n2, nrm, nrc, rn0, r2, hh, hn, rn, rn2 = [
+                small(n) for n in ("Ssum", "nz", "sq", "nq", "nqe", "n2", "nrm", "nrc", "rn0", "r2", "hh", "hn", "rn", "rn2")
+            ]
             SH = D - PACK + 1
-            HG = NG // 2
+            CUT = [0, 4, NG]
             queues = [nc.sync, nc.scalar, nc.sync, nc.scalar]
             for h in range(2):
+                gs = slice(CUT[h], CUT[h + 1])
                 for t in range(PACK):
-                    queues[t].dma_start(out=F[t:P:PACK, h * HG:(h + 1) * HG, :], in_=feat_v[:, h * HG:(h + 1) * HG, :])
-            nc.sync.dma_start(out=Fraw[:], in_=feat_n)
-            for t in range(PACK):
-                queues[t].dma_start(out=Fs[t:P:PACK, :, 0:SH], in_=feat_v[:, :, t:t + SH])
+                    queues[t].dma_start(out=F[t:P:PACK, gs, :], in_=feat_v[:, gs, :])
+                for t in range(PACK):
+                    queues[t].dma_start(out=Fs[t:P:PACK, gs, 0:SH], in_=feat_v[:, gs, t:t + SH])
+                if h == 0:
+                    nc.sync.dma_start(out=Fraw[:], in_=feat_n)
             nc.gpsimd.dma_start(out=bb[:], in_=b.partition_broadcast(P))
             load_w2(0)
             load_w2(1)
-            load_wn(Wb, HD, 0)
+            for q in range(PACK):
+                load_wn(Wb, HD, 0, q)
             load_w2(2)
-            load_w2(3)
             make_identity(nc, ident_bf[:])
             make_identity(nc, ident_f[:])
             nc.gpsimd.tensor_copy(out=mask_a[:], in_=ident_bf[:])
@@ -356,28 +358,28 @@ def tile_bcnnresnet_kernel(tc, feat, W, b, out):
             FI = Fs[:, :, 0:SH:PACK]
 
             def head_count(h):
-                gs = slice(h * HG, (h + 1) * HG)
+                gs = slice(CUT[h], CUT[h + 1])
                 nc.vector.tensor_scalar(out=nonzero[:, gs, :], in0=F[:, gs, :], scalar1=0.0, scalar2=None, op0=ALU.not_equal)
                 nc.vector.tensor_reduce(out=nz[:, gs], in_=nonzero[:, gs, :], axis=AX.X, op=ALU.add)
 
             def head_abs_i(h):
-                gs = slice(h * HG, (h + 1) * HG)
-                nc.vector.tensor_scalar(out=FIn[:, gs, :], in0=FI[:, gs, :], scalar1=-1.0, scalar2=None, op0=ALU.mult)
-                nc.vector.tensor_tensor(out=AI[:, gs, :], in0=FI[:, gs, :], in1=FIn[:, gs, :], op=ALU.max)
+                gs = slice(CUT[h], CUT[h + 1])
+                nc.vector.tensor_scalar(out=FIn[:, gs, :], in0=Fs[:, gs, 0:SH:PACK], scalar1=-1.0, scalar2=None, op0=ALU.mult)
+                nc.vector.tensor_tensor(out=AI[:, gs, :], in0=Fs[:, gs, 0:SH:PACK], in1=FIn[:, gs, :], op=ALU.max)
 
             def head_norm_v(h):
-                gs = slice(h * HG, (h + 1) * HG)
+                gs = slice(CUT[h], CUT[h + 1])
                 nc.vector.tensor_tensor(out=sq[:, gs], in0=Ssum[:, gs], in1=Ssum[:, gs], op=ALU.mult)
                 nc.vector.tensor_tensor(out=nq[:, gs], in0=nz[:, gs], in1=nz[:, gs], op=ALU.mult)
                 nc.vector.tensor_scalar(out=nqe[:, gs], in0=nq[:, gs], scalar1=EPS_SQRT, scalar2=None, op0=ALU.mult)
                 nc.vector.tensor_tensor(out=n2[:, gs], in0=sq[:, gs], in1=nqe[:, gs], op=ALU.add)
 
             def head_norm_s(h):
-                gs = slice(h * HG, (h + 1) * HG)
+                gs = slice(CUT[h], CUT[h + 1])
                 nc.scalar.activation(out=nrm[:, gs], in_=n2[:, gs], func=ACT.Sqrt)
 
             def head_scale(h):
-                gs = slice(h * HG, (h + 1) * HG)
+                gs = slice(CUT[h], CUT[h + 1])
                 nc.vector.tensor_scalar(out=nrc[:, gs], in0=nrm[:, gs], scalar1=EPS_NORM, scalar2=None, op0=ALU.max)
                 nc.vector.reciprocal(out=rn0[:, gs], in_=nrc[:, gs])
                 nc.vector.tensor_tensor(out=r2[:, gs], in0=rn0[:, gs], in1=rn0[:, gs], op=ALU.mult)
@@ -387,35 +389,36 @@ def tile_bcnnresnet_kernel(tc, feat, W, b, out):
                 nc.vector.tensor_tensor(out=rn2[:, gs], in0=rn[:, gs], in1=rn[:, gs], op=ALU.mult)
                 nc.vector.tensor_scalar(out=beta[:, gs], in0=rn2[:, gs], scalar1=EPS_SQRT, scalar2=None, op0=ALU.mult)
                 nc.vector.tensor_tensor(
-                    out=alpha[:, gs, :], in0=AI[:, gs, :], in1=rn2[:, gs].unsqueeze(2).to_broadcast([P, HG, NM]), op=ALU.mult
+                    out=alpha[:, gs, :], in0=AI[:, gs, :], in1=rn2[:, gs].unsqueeze(2).to_broadcast([P, CUT[h + 1] - CUT[h], NM]), op=ALU.mult
                 )
 
             def head_abs(g0, g1):
                 for g in range(g0, g1):
                     nc.scalar.activation(out=A[:, g, :], in_=F[:, g, :], func=ACT.Abs, accum_out=Ssum[:, g:g + 1])
 
-            head_abs(0, 8)
+            head_abs(0, 4)
             head_count(0)
             head_norm_v(0)
             nc.scalar.activation(out=Fn[:], in_=Fraw[:], func=ACT.Sign)
-            nc.gpsimd.tensor_copy(out=Fm[:], in_=Fn[:, :, 0:HD])
             head_norm_s(0)
-            stage_tab_t(0)
             head_abs_i(0)
-            head_abs(8, 16)
             head_scale(0)
+            nc.gpsimd.tensor_copy(out=Fm[:], in_=Fn[:, :, 0:HD])
+            stage_tab_t(0)
+            head_abs(4, 9)
+            stage_sqrt(0, 0)
+            head_abs(9, 16)
+            head_count(1)
+            head_norm_v(1)
+            head_norm_s(1)
             stage_tab_s(0)
             stage_tab_t(K16)
             nc.scalar.activation(out=SI[:], in_=FI[:, :, 0:HM], func=ACT.Sign)
-            head_count(1)
-            head_norm_v(1)
-            stage_sqrt(0, 0)
-            stage_sqrt(0, 1)
-            head_norm_s(1)
-            stage_tab_s(K16)
-            stage_sqrt(1, 0)
             head_abs_i(1)
             head_scale(1)
+            stage_sqrt(1, 0)
+            stage_sqrt(0, 1)
+            stage_tab_s(K16)
             stage_sqrt(0, 2)
             stage_sqrt(0, 3)
             stage_sign(0, 0)
@@ -424,8 +427,8 @@ def tile_bcnnresnet_kernel(tc, feat, W, b, out):
             stage_t(0, 0)
             nc.scalar.activation(out=SIp[:], in_=FI[:, :, HM:NM].rearrange("q g m -> q m g").unsqueeze(3).to_broadcast([P, HM, NG, 2]), func=ACT.Sign)
 
-        late[1] = ctx.enter_context(tc.tile_pool(name="xrpool", bufs=4))
-        late[0] = ctx.enter_context(tc.tile_pool(name="xmpool", bufs=10))
+        late[1] = ctx.enter_context(tc.tile_pool(name="xrpool", bufs=6))
+        late[0] = ctx.enter_context(tc.tile_pool(name="xmpool", bufs=11))
         stage_w2mix(0)
         stage_sign(0, 2)
         stage_sign(0, 3)
@@ -442,11 +445,13 @@ def tile_bcnnresnet_kernel(tc, feat, W, b, out):
             old = plan.get(s - 1, [])
             old2 = plan.get(s - 2, [])
             if s % CH == 0:
-                load_w2(s // CH + 4)
-            if s == 0:
-                load_wn(Wb, HD, HD)
-            if s == 2:
-                load_wn(Wa, 0, 0)
+                load_w2(s // CH + 3)
+            for q in range(2 * PACK):
+                if s == 3 * q // 4:
+                    if q < PACK:
+                        load_wn(Wb, HD, HD, q)
+                    else:
+                        load_wn(Wa, 0, 0, q - PACK)
             for w, h in old2:
                 stage_mx1(w, h)
             stage_mx2(s - 1)
@@ -487,8 +492,8 @@ def tile_bcnnresnet_kernel(tc, feat, W, b, out):
             stage_t(s + 1, 1)
             if s % 2 == 1:
                 stage_w2mix((s + 3) // 2)
-            stage_q2(s, 0)
             stage_q2(s, 1)
+            stage_q2(s, 0)
         stage_mx2(NS - 1)
         for w, h in plan[NS - 2]:
             stage_mx1(w, h)

@@ -25,7 +25,7 @@ NS = HM + 2
 CH = 2
 EPS_SQRT = 1e-10
 EPS_NORM = 1e-12
-START_R, START_M = 4, 9
+START_R, START_M = 4, 10
 FLOPS = 2 * B * D * D * C
 
 
@@ -70,25 +70,22 @@ def tile_bcnnresnet_kernel(tc, feat, W, b, out):
 
         beta = const.tile([P, NG], F32, name="beta")
 
-        wr_tiles, wp_tiles = {}, {}
+        wr_tiles = {}
 
         def load_w2(ch):
-            s0 = ch * CH
-            if s0 >= NS:
+            if ch * CH >= NS:
                 return
-            if s0 < HM:
-                Wr = wrpool.tile([P, PACK, CH, D], BF16, name="Wr")
-                for e in range(CH):
-                    for t in range(PACK):
-                        nc.sync.dma_start(out=Wr[t:P:PACK, :, e, :], in_=W_v[t, s0 + e])
-                wr_tiles[ch] = Wr
-            if s0 == 0:
-                return
-            Wp = wrpool.tile([P, PACK, CH, HD], BF16, name="Wp")
+            Wr = wrpool.tile([P, PACK, CH, D], BF16, name="Wr")
+            lo, hi = max(0, OCT * ch - OCT), OCT * ch + OCT
+            nc.gpsimd.memset(Wr[:, :, :, lo:min(hi, HD)], 0.0)
             for e in range(CH):
+                s = ch * CH + e
                 for t in range(PACK):
-                    nc.sync.dma_start(out=Wp[t:P:PACK, :, e, :], in_=W_v[t, HM - 2 + s0 + e, :, :, HD:D])
-            wp_tiles[ch] = Wp
+                    if s < HM:
+                        nc.sync.dma_start(out=Wr[t:P:PACK, :, e, hi:D], in_=W_v[t, s, :, :, hi:D])
+                    if lo > 0:
+                        nc.sync.dma_start(out=Wr[t:P:PACK, :, e, 0:lo], in_=W_v[t, HM - 2 + s, :, :, HD:HD + lo])
+            wr_tiles[ch] = Wr
 
         def load_wn(dst, j0, i0, q):
             cs = slice(q * NL, q * NL + NL)
@@ -188,21 +185,6 @@ def tile_bcnnresnet_kernel(tc, feat, W, b, out):
             nc.vector.quantize_mx(out=Xc[:].bitcast(FP8X4), scales=Xs[:], in_=g_tiles[s][:, h * PACK * B:(h + 1) * PACK * B])
             xb_tiles[(s, h)] = (Xc, Xs)
 
-        def stage_w2mix(k):
-            if k > HD // OCT:
-                return
-            s = 2 * k
-            e = slice(s % CH, s % CH + 2)
-            Wp = wp_tiles.get(s // CH)
-            if s >= HM:
-                nc.gpsimd.memset(Wp[:, :, e, HD - OCT:HD], 0.0)
-                return
-            Wr = wr_tiles[s // CH]
-            lo = OCT * k
-            nc.gpsimd.memset(Wr[:, :, e, max(0, lo - OCT):lo + OCT], 0.0)
-            if k >= 2:
-                nc.scalar.copy(out=Wr[:, :, e, 0:lo - OCT], in_=Wp[:, :, e, 0:lo - OCT])
-
         def stage_w2t(s):
             if s >= NS:
                 return
@@ -210,8 +192,7 @@ def tile_bcnnresnet_kernel(tc, feat, W, b, out):
             for h in range(2 if s < HM else 1):
                 for gc in range(PACK):
                     o = (h * PACK + gc) * P
-                    src = wr_tiles[s // CH] if s < HM else wp_tiles[s // CH]
-                    nc.tensor.transpose(out=ps[:, o:o + P], in_=src[:, gc, s % CH, h * HD:(h + 1) * HD], identity=ident_bf[:])
+                    nc.tensor.transpose(out=ps[:, o:o + P], in_=wr_tiles[s // CH][:, gc, s % CH, h * HD:(h + 1) * HD], identity=ident_bf[:])
             wt_tiles[s] = ps
 
         def stage_w2c(s):
@@ -329,11 +310,11 @@ def tile_bcnnresnet_kernel(tc, feat, W, b, out):
             def small(name):
                 return pro.tile([P, NG], F32, name=name)
 
-            Ssum, nz, sq, nq, nqe, n2, nrm, nrc, rn0, r2, hh, hn, rn, rn2 = [
-                small(n) for n in ("Ssum", "nz", "sq", "nq", "nqe", "n2", "nrm", "nrc", "rn0", "r2", "hh", "hn", "rn", "rn2")
-            ]
+            Ssum, nz, sq, nqe, n2, nm, rn2 = [small(n) for n in ("Ssum", "nz", "sq", "nqe", "n2", "nm", "rn2")]
             SH = D - PACK + 1
-            CUT = [0, 4, NG]
+            nc.gpsimd.memset(one[:], 1.0)
+            nc.scalar.activation(out=one[:], in_=one[:], func=ACT.Sqrt)
+            CUT = [0, 8, NG]
             queues = [nc.sync, nc.scalar, nc.sync, nc.scalar]
             for h in range(2):
                 gs = slice(CUT[h], CUT[h + 1])
@@ -353,40 +334,27 @@ def tile_bcnnresnet_kernel(tc, feat, W, b, out):
             make_identity(nc, ident_f[:])
             nc.gpsimd.tensor_copy(out=mask_a[:], in_=ident_bf[:])
             nc.gpsimd.memset(mask_b[:], 0.0)
-            nc.vector.memset(one[:], 1.0)
-            nc.scalar.activation(out=one[:], in_=one[:], func=ACT.Sqrt)
             FI = Fs[:, :, 0:SH:PACK]
 
             def head_count(h):
                 gs = slice(CUT[h], CUT[h + 1])
                 nc.vector.tensor_scalar(out=nonzero[:, gs, :], in0=F[:, gs, :], scalar1=0.0, scalar2=None, op0=ALU.not_equal)
-                nc.vector.tensor_reduce(out=nz[:, gs], in_=nonzero[:, gs, :], axis=AX.X, op=ALU.add)
+                for w in (128, 64, 32, 16):
+                    nc.vector.tensor_tensor(out=nonzero[:, gs, 0:w], in0=nonzero[:, gs, 0:w], in1=nonzero[:, gs, w:2 * w], op=ALU.add)
+                nc.vector.tensor_reduce(out=nz[:, gs], in_=nonzero[:, gs, 0:16], axis=AX.X, op=ALU.add)
 
             def head_abs_i(h):
                 gs = slice(CUT[h], CUT[h + 1])
                 nc.vector.tensor_scalar(out=FIn[:, gs, :], in0=Fs[:, gs, 0:SH:PACK], scalar1=-1.0, scalar2=None, op0=ALU.mult)
                 nc.vector.tensor_tensor(out=AI[:, gs, :], in0=Fs[:, gs, 0:SH:PACK], in1=FIn[:, gs, :], op=ALU.max)
 
-            def head_norm_v(h):
-                gs = slice(CUT[h], CUT[h + 1])
-                nc.vector.tensor_tensor(out=sq[:, gs], in0=Ssum[:, gs], in1=Ssum[:, gs], op=ALU.mult)
-                nc.vector.tensor_tensor(out=nq[:, gs], in0=nz[:, gs], in1=nz[:, gs], op=ALU.mult)
-                nc.vector.tensor_scalar(out=nqe[:, gs], in0=nq[:, gs], scalar1=EPS_SQRT, scalar2=None, op0=ALU.mult)
-                nc.vector.tensor_tensor(out=n2[:, gs], in0=sq[:, gs], in1=nqe[:, gs], op=ALU.add)
-
-            def head_norm_s(h):
-                gs = slice(CUT[h], CUT[h + 1])
-                nc.scalar.activation(out=nrm[:, gs], in_=n2[:, gs], func=ACT.Sqrt)
-
             def head_scale(h):
                 gs = slice(CUT[h], CUT[h + 1])
-                nc.vector.tensor_scalar(out=nrc[:, gs], in0=nrm[:, gs], scalar1=EPS_NORM, scalar2=None, op0=ALU.max)
-                nc.vector.reciprocal(out=rn0[:, gs], in_=nrc[:, gs])
-                nc.vector.tensor_tensor(out=r2[:, gs], in0=rn0[:, gs], in1=rn0[:, gs], op=ALU.mult)
-                nc.vector.tensor_tensor(out=hh[:, gs], in0=r2[:, gs], in1=n2[:, gs], op=ALU.mult)
-                nc.vector.tensor_scalar(out=hn[:, gs], in0=hh[:, gs], scalar1=-0.5, scalar2=1.5, op0=ALU.mult, op1=ALU.add)
-                nc.vector.tensor_tensor(out=rn[:, gs], in0=rn0[:, gs], in1=hn[:, gs], op=ALU.mult)
-                nc.vector.tensor_tensor(out=rn2[:, gs], in0=rn[:, gs], in1=rn[:, gs], op=ALU.mult)
+                nc.vector.tensor_tensor(out=sq[:, gs], in0=Ssum[:, gs], in1=Ssum[:, gs], op=ALU.mult)
+                nc.vector.scalar_tensor_tensor(out=nqe[:, gs], in0=nz[:, gs], scalar=EPS_SQRT, in1=nz[:, gs], op0=ALU.mult, op1=ALU.mult)
+                nc.vector.tensor_tensor(out=n2[:, gs], in0=sq[:, gs], in1=nqe[:, gs], op=ALU.add)
+                nc.vector.tensor_scalar(out=nm[:, gs], in0=n2[:, gs], scalar1=EPS_NORM * EPS_NORM, scalar2=None, op0=ALU.max)
+                nc.vector.reciprocal(out=rn2[:, gs], in_=nm[:, gs])
                 nc.vector.tensor_scalar(out=beta[:, gs], in0=rn2[:, gs], scalar1=EPS_SQRT, scalar2=None, op0=ALU.mult)
                 nc.vector.tensor_tensor(
                     out=alpha[:, gs, :], in0=AI[:, gs, :], in1=rn2[:, gs].unsqueeze(2).to_broadcast([P, CUT[h + 1] - CUT[h], NM]), op=ALU.mult
@@ -396,51 +364,47 @@ def tile_bcnnresnet_kernel(tc, feat, W, b, out):
                 for g in range(g0, g1):
                     nc.scalar.activation(out=A[:, g, :], in_=F[:, g, :], func=ACT.Abs, accum_out=Ssum[:, g:g + 1])
 
-            head_abs(0, 4)
+            head_abs(0, 8)
             head_count(0)
-            head_norm_v(0)
-            nc.scalar.activation(out=Fn[:], in_=Fraw[:], func=ACT.Sign)
-            head_norm_s(0)
             head_abs_i(0)
             head_scale(0)
-            nc.gpsimd.tensor_copy(out=Fm[:], in_=Fn[:, :, 0:HD])
-            stage_tab_t(0)
-            head_abs(4, 9)
-            stage_sqrt(0, 0)
-            head_abs(9, 16)
-            head_count(1)
-            head_norm_v(1)
-            head_norm_s(1)
-            stage_tab_s(0)
+            nc.scalar.activation(out=Fn[:], in_=Fraw[:], func=ACT.Sign)
             stage_tab_t(K16)
             nc.scalar.activation(out=SI[:], in_=FI[:, :, 0:HM], func=ACT.Sign)
-            head_abs_i(1)
-            head_scale(1)
-            stage_sqrt(1, 0)
+            head_abs(8, 10)
+            nc.gpsimd.tensor_scalar(out=Fm[:], in0=Fn[:, :, 0:HD], scalar1=1.0, scalar2=0.0, op0=ALU.mult, op1=ALU.add)
+            stage_sqrt(0, 0)
             stage_sqrt(0, 1)
             stage_tab_s(K16)
-            stage_sqrt(0, 2)
-            stage_sqrt(0, 3)
+            stage_tab_t(0)
+            head_abs(10, 16)
+            stage_tab_s(0)
             stage_sign(0, 0)
+            head_count(1)
             stage_sign(0, 1)
             stage_t(0, 2)
             stage_t(0, 0)
+            head_abs_i(1)
+            head_scale(1)
+            stage_e(0, 2)
+            stage_sqrt(1, 0)
+            stage_sqrt(0, 2)
+            stage_sqrt(0, 3)
+            stage_e(0, 0)
+            stage_sqrt(1, 1)
             nc.scalar.activation(out=SIp[:], in_=FI[:, :, HM:NM].rearrange("q g m -> q m g").unsqueeze(3).to_broadcast([P, HM, NG, 2]), func=ACT.Sign)
 
         late[1] = ctx.enter_context(tc.tile_pool(name="xrpool", bufs=6))
-        late[0] = ctx.enter_context(tc.tile_pool(name="xmpool", bufs=11))
-        stage_w2mix(0)
+        late[0] = ctx.enter_context(tc.tile_pool(name="xmpool", bufs=12))
         stage_sign(0, 2)
         stage_sign(0, 3)
         stage_t(0, 3)
         stage_t(0, 1)
         stage_w2t(0)
-        stage_sqrt(1, 1)
         stage_w2c(0)
         stage_w2t(1)
         stage_sqrt(1, 2)
         stage_sqrt(1, 3)
-        stage_w2mix(1)
         for s in range(NS):
             old = plan.get(s - 1, [])
             old2 = plan.get(s - 2, [])
@@ -455,7 +419,8 @@ def tile_bcnnresnet_kernel(tc, feat, W, b, out):
             for w, h in old2:
                 stage_mx1(w, h)
             stage_mx2(s - 1)
-            stage_e(s, 2)
+            if s > 0:
+                stage_e(s, 2)
             stage_sign(s + 1, 0)
             for w, h in old:
                 stage_wq(h, w)
@@ -473,7 +438,8 @@ def tile_bcnnresnet_kernel(tc, feat, W, b, out):
             stage_t(s + 1, 2)
             stage_idle(s - 1, 2)
             stage_wq(2, s)
-            stage_e(s, 0)
+            if s > 0:
+                stage_e(s, 0)
             stage_sign(s + 1, 2)
             stage_w2t(s + 2)
             for w, h in plan[s]:
@@ -488,29 +454,26 @@ def tile_bcnnresnet_kernel(tc, feat, W, b, out):
             stage_mix(plan.get(s + 1, []))
             stage_idle(s - 1, 2)
             stage_t(s + 1, 0)
+            if s == NS - 1:
+                for w, h in plan[s]:
+                    stage_wq(h, w)
             stage_q(s)
             stage_t(s + 1, 1)
-            if s % 2 == 1:
-                stage_w2mix((s + 3) // 2)
             stage_q2(s, 1)
             stage_q2(s, 0)
         stage_mx2(NS - 1)
         for w, h in plan[NS - 2]:
             stage_mx1(w, h)
         for w, h in plan[NS - 1]:
-            stage_wq(h, w)
             stage_mx1(w, h)
 
         accS = zpool.tile([P, B], F32, name="Z")
-        nc.vector.tensor_copy(out=accS[:], in_=acc[:])
-        pso = tps.tile([P, B], F32, name="pso", tag="t")
-        for nb in range(B // P):
-            nc.tensor.transpose(out=pso[:, nb * P:(nb + 1) * P], in_=accS[:, nb * P:(nb + 1) * P], identity=ident_f[:])
         res = zpool.tile([P, B // P, C], F32, name="Z")
-        nc.vector.tensor_tensor(
-            out=res[:],
-            in0=pso[:].rearrange("p (nb c) -> p nb c", c=C),
-            in1=bb[:].unsqueeze(1).to_broadcast([P, B // P, C]),
-            op=ALU.add,
-        )
-        nc.sync.dma_start(out=out.rearrange("(nb p) c -> p nb c", p=P), in_=res[:])
+        out_v = out.rearrange("(nb p) c -> p nb c", p=P)
+        for nb in range(B // P):
+            cs = slice(nb * P, (nb + 1) * P)
+            nc.scalar.copy(out=accS[:, cs], in_=acc[:, cs])
+            pso = tps.tile([P, P], F32, name="pso", tag="t")
+            nc.tensor.transpose(out=pso[:], in_=accS[:, cs], identity=ident_f[:])
+            nc.vector.tensor_tensor(out=res[:, nb, :], in0=pso[:], in1=bb[:], op=ALU.add)
+            nc.sync.dma_start(out=out_v[:, nb, :], in_=res[:, nb, :])

from contextlib import ExitStack

import concourse.mybir as mybir
from concourse.masks import make_identity

FP8X4 = mybir.dt.float8_e4m3fn_x4
BF16 = mybir.dt.bfloat16
F32 = mybir.dt.float32
U32 = mybir.dt.uint32
U8 = mybir.dt.uint8
ACT = mybir.ActivationFunctionType
ALU = mybir.AluOpType
AX = mybir.AxisListType

B, D, C = 512, 256, 128
P = 128
PACK = 4
NL = P // PACK
NG = B // NL
NM = D // PACK
HD = D // 2
HM = NM // 2
OCT = 8
NS = HM + 2
CH = 2
EPS_SQRT = 1e-10
EPS_NORM = 1e-12
START_R, START_M = 4, 10
FLOPS = 2 * B * D * D * C


def tile_bcnnresnet_kernel(tc, feat, W, b, out):
    nc = tc.nc
    with ExitStack() as ctx:
        const = ctx.enter_context(tc.tile_pool(name="const", bufs=1))
        zpool = ctx.enter_context(tc.tile_pool(name="zpool", bufs=3))
        gpool = ctx.enter_context(tc.tile_pool(name="gpool", bufs=1))
        xapool = ctx.enter_context(tc.tile_pool(name="xapool", bufs=2))
        wrpool = ctx.enter_context(tc.tile_pool(name="wrpool", bufs=3))
        wgpool = ctx.enter_context(tc.tile_pool(name="wgpool", bufs=2))
        wg2pool = ctx.enter_context(tc.tile_pool(name="wg2pool", bufs=2))
        wcpool = ctx.enter_context(tc.tile_pool(name="wcpool", bufs=3))
        wc2pool = ctx.enter_context(tc.tile_pool(name="wc2pool", bufs=2))
        tabp = ctx.enter_context(tc.tile_pool(name="tabp", bufs=2))
        accp = ctx.enter_context(tc.psum_pool(name="accp", bufs=1))
        tps = ctx.enter_context(tc.psum_pool(name="tps", bufs=4))
        wps = ctx.enter_context(tc.psum_pool(name="wps", bufs=1))
        aux = ctx.enter_context(tc.psum_pool(name="aux", bufs=1))
        dps = ctx.enter_context(tc.psum_pool(name="dps", bufs=1))

        feat_v = feat.rearrange("(g nl) j -> nl g j", nl=NL)
        feat_n = feat.rearrange("(tl n) j -> n tl j", n=P)
        W_v = W.rearrange("(gc cl) (m t j) -> t m cl gc j", cl=NL, t=PACK, j=D)
        W_n = W.rearrange("c (j i) -> j c i", i=D)

        A = const.tile([P, NG, D], BF16, name="A")
        SI = const.tile([P, NG, HM], F32, name="SI")
        SIp = const.tile([P, HM, NG, 2], BF16, name="SIp")
        alpha = const.tile([P, NG, NM], F32, name="alpha")
        bb = const.tile([P, C], BF16, name="bb")
        ident_bf = const.tile([P, P], BF16, name="ident_bf")
        ident_f = const.tile([P, P], F32, name="ident_f")
        T16 = const.tile([P, B, 2], BF16, name="T16")
        Fn = const.tile([P, B // P, D], BF16, name="Fn")
        Fm = const.tile([P, B // P, HD], BF16, name="Fm")
        Wa = const.tile([P, C, HD], BF16, name="Wa")
        Wb = const.tile([P, C, D], BF16, name="Wb")
        mask_a = const.tile([P, P], BF16, name="mask_a")
        mask_b = const.tile([P, P], BF16, name="mask_b")

        beta = const.tile([P, NG], F32, name="beta")

        wr_tiles = {}

        def load_w2(ch):
            if ch * CH >= NS:
                return
            Wr = wrpool.tile([P, PACK, CH, D], BF16, name="Wr")
            lo, hi = max(0, OCT * ch - OCT), OCT * ch + OCT
            nc.gpsimd.memset(Wr[:, :, :, lo:min(hi, HD)], 0.0)
            for e in range(CH):
                s = ch * CH + e
                for t in range(PACK):
                    if s < HM:
                        nc.sync.dma_start(out=Wr[t:P:PACK, :, e, hi:D], in_=W_v[t, s, :, :, hi:D])
                    if lo > 0:
                        nc.sync.dma_start(out=Wr[t:P:PACK, :, e, 0:lo], in_=W_v[t, HM - 2 + s, :, :, HD:HD + lo])
            wr_tiles[ch] = Wr

        def load_wn(dst, j0, i0, q):
            cs = slice(q * NL, q * NL + NL)
            nc.sync.dma_start(out=dst[:, cs, i0:i0 + HD], in_=W_n[j0:j0 + HD, cs, i0:i0 + HD])

        acc = accp.tile([P, B], F32, name="acc")

        z_tiles, t_tiles, g_tiles, xa_tiles, xb_tiles = {}, {}, {}, {}, {}
        wt_tiles, wg_tiles, wq_tiles, tt_tiles, tabs = {}, {}, {}, {}, {HD // OCT: T16}
        mix_tiles, mask_k = {}, [0]
        passes, late = [], {}
        N_PASS = 4 * HM + 2 * (NS - HM)

        def stage_tab_t(k):
            if 0 < k < HD // OCT:
                cs = slice(OCT * (k - 1), OCT * k)
                nc.gpsimd.tensor_copy(out=Fm[:, :, cs], in_=Fn[:, :, HD + OCT * (k - 1):HD + OCT * k])
            ps = aux.tile([P, B], BF16, name="pst", tag="x")
            for tl in range(B // P):
                src = Fn[:, tl, HD:D] if k == HD // OCT else Fm[:, tl, :]
                nc.tensor.transpose(out=ps[:, tl * P:(tl + 1) * P], in_=src, identity=ident_bf[:])
            tt_tiles[k] = ps

        def stage_tab_s(k):
            if k not in tt_tiles:
                return
            if k not in tabs:
                tabs[k] = tabp.tile([P, B, 2], BF16, name="T")
            nc.scalar.copy(out=tabs[k][:], in_=tt_tiles.pop(k)[:].unsqueeze(2).to_broadcast([P, B, 2]))

        def stage_sqrt(s, q):
            if s >= NS:
                return
            if q == 0:
                z_tiles[s] = zpool.tile([P, NG, D], BF16, name="Z")
            Z = z_tiles[s]
            lo = OCT * (s // 2)
            for g in range(4 * q, 4 * q + 4):
                if s < HM:
                    nc.scalar.activation(out=Z[:, g, lo:D], in_=A[:, g, lo:D], func=ACT.Sqrt, bias=beta[:, g:g + 1], scale=alpha[:, g, s:s + 1])
                if s >= 2:
                    m = HM - 2 + s
                    nc.scalar.activation(out=Z[:, g, 0:lo], in_=A[:, g, HD:HD + lo], func=ACT.Sqrt, bias=beta[:, g:g + 1], scale=alpha[:, g, m:m + 1])

        def stage_sign(s, q):
            if s >= HM:
                return
            Z = z_tiles[s]
            lo = OCT * (s // 2)
            for g in range(4 * q, 4 * q + 4):
                nc.vector.tensor_scalar(out=Z[:, g, lo:D], in0=Z[:, g, lo:D], scalar1=SI[:, g, s:s + 1], scalar2=None, op0=ALU.mult)

        def stage_sign2(s):
            if s < 2 or s >= NS:
                return
            lo = OCT * (s // 2)
            V = z_tiles[s][:, :, 0:lo].rearrange("p g (h w) -> p g h w", w=2)
            nc.vector.tensor_tensor(out=V, in0=V, in1=SIp[:, s - 2, :, :].unsqueeze(2).to_broadcast([P, NG, lo // 2, 2]), op=ALU.mult)

        def stage_t(s, j):
            if s >= NS or (s >= HM and j >= 2):
                return
            Z = z_tiles[s]
            c0 = (j // 2) * HD
            ps = tps.tile([P, 8 * P], BF16, name="ps", tag="t")
            for gg in range(8):
                nc.tensor.transpose(out=ps[:, gg * P:(gg + 1) * P], in_=Z[:, 8 * (j % 2) + gg, c0:c0 + HD], identity=ident_bf[:])
            t_tiles[(s, j)] = ps

        def stage_e(s, j):
            if s >= HM and j >= 2:
                return
            if s not in g_tiles:
                g_tiles[s] = gpool.tile([P, 2 * NG * P], BF16, name="G", align_bytes=64)
            T = tabs[s // 2] if j < 2 else T16
            h = j % 2
            nc.vector.tensor_tensor(
                out=g_tiles[s][:, j * 1024:(j + 1) * 1024].rearrange("p (n a b) -> p n a b", a=2, b=2),
                in0=t_tiles.pop((s, j))[:].rearrange("p (n a b) -> p n a b", a=2, b=2),
                in1=T[:, h * 256:(h + 1) * 256, :].unsqueeze(2).to_broadcast([P, 256, 2, 2]),
                op=ALU.mult,
            )

        def stage_q(s):
            n = 2 * B if s < HM else B
            Xc = xapool.tile([P, 2 * B], U32, name="Xc", align_bytes=64)
            Xs = xapool.tile([P, 2 * B], U8, name="Xs", align_bytes=64)
            nc.vector.quantize_mx(out=Xc[:, 0:n].bitcast(FP8X4), scales=Xs[:, 0:n], in_=g_tiles[s][:, 0:PACK * n])
            xa_tiles[s] = (Xc, Xs)

        def stage_q2(s, h):
            if s >= HM and h == 1:
                return
            pool = late[h]
            Xc = pool.tile([P, B], U32, name="Yc", align_bytes=64)
            Xs = pool.tile([P, B], U8, name="Ys", align_bytes=64)
            nc.vector.quantize_mx(out=Xc[:].bitcast(FP8X4), scales=Xs[:], in_=g_tiles[s][:, h * PACK * B:(h + 1) * PACK * B])
            xb_tiles[(s, h)] = (Xc, Xs)

        def stage_w2t(s):
            if s >= NS:
                return
            ps = wps.tile([P, 8 * P], BF16, name="wt")
            for h in range(2 if s < HM else 1):
                for gc in range(PACK):
                    o = (h * PACK + gc) * P
                    nc.tensor.transpose(out=ps[:, o:o + P], in_=wr_tiles[s // CH][:, gc, s % CH, h * HD:(h + 1) * HD], identity=ident_bf[:])
            wt_tiles[s] = ps

        def stage_w2c(s):
            if s >= NS:
                return
            n = 8 * P if s < HM else 4 * P
            Wg = wg2pool.tile([P, 8 * P], BF16, name="Wg2", align_bytes=64)
            nc.scalar.copy(out=Wg[:, 0:n], in_=wt_tiles.pop(s)[:, 0:n])
            wg_tiles[(2, s)] = Wg

        def mixes(s, h):
            return h == 0 and (s // 2) % 4 != 0

        def stage_mix(todo):
            todo = [s for s, h in todo if mixes(s, h)]
            if not todo:
                return
            ps = aux.tile([P, 2, 4 * P], BF16, name="mix", tag="x")
            for n, s in enumerate(todo):
                k = s // 2
                while mask_k[0] < k:
                    cs = slice(OCT * mask_k[0], OCT * (mask_k[0] + 1))
                    nc.gpsimd.tensor_copy(out=mask_b[:, cs], in_=ident_bf[:, cs])
                    nc.gpsimd.memset(mask_a[:, cs], 0.0)
                    mask_k[0] += 1
                o = ps[:, n, :].rearrange("p (c w) -> p c w", w=4)
                nc.tensor.matmul(out=o, lhsT=mask_a[:], rhs=Wa[:, :, 4 * s:4 * s + 4], start=True, stop=False)
                nc.tensor.matmul(out=o, lhsT=mask_b[:], rhs=Wb[:, :, HD - OCT + 4 * s:HD - OCT + 4 * s + 4], start=False, stop=True)
                mix_tiles[s] = (ps, n)

        def stage_w1c(s, h):
            Wg = wgpool.tile([P, 4 * P], BF16, name="Wg1%d" % h, align_bytes=64)
            wg_tiles[(h, s)] = Wg
            if mixes(s, h):
                ps, n = mix_tiles.pop(s)
                nc.scalar.copy(out=Wg[:], in_=ps[:, n, :])
                return
            dst = Wg[:].bitcast(F32).rearrange("p (c w) -> p c w", w=2)
            Va, Vb = Wa[:].bitcast(F32), Wb[:].bitcast(F32)
            if h == 1:
                nc.scalar.copy(out=dst, in_=Vb[:, :, 2 * s:2 * s + 2])
                return
            b0 = (HD - OCT) // 2 + 2 * s
            lo = OCT * (s // 2)
            if lo <= HD // 2:
                nc.scalar.copy(out=dst, in_=Va[:, :, 2 * s:2 * s + 2])
                if lo > 0:
                    nc.scalar.copy(out=dst[0:lo], in_=Vb[0:lo, :, b0:b0 + 2])
            else:
                nc.scalar.copy(out=dst, in_=Vb[:, :, b0:b0 + 2])
                if lo < HD:
                    nc.scalar.copy(out=dst[lo:P], in_=Va[lo:P, :, 2 * s:2 * s + 2])

        def stage_wq(kind, s):
            if (kind, s) not in wg_tiles:
                return
            n = 2 * P if kind == 2 and s < HM else P
            pool, cols = (wc2pool, 2 * P) if kind == 2 else (wcpool, P)
            Wc = pool.tile([P, cols], U32, name="Wc%d" % kind, align_bytes=64)
            Ws = pool.tile([P, cols], U8, name="Ws%d" % kind, align_bytes=64)
            nc.vector.quantize_mx(out=Wc[:, 0:n].bitcast(FP8X4), scales=Ws[:, 0:n], in_=wg_tiles.pop((kind, s))[:, 0:PACK * n])
            wq_tiles[(kind, s)] = (Wc, Ws)

        def mx_pass(dst, w, wcol, x, xcol, start, stop):
            nc.tensor.matmul_mx(
                out=dst[:],
                lhsT=w[0][:, wcol:wcol + P].bitcast(FP8X4),
                lhsT_scale=w[1][:, wcol:wcol + P],
                rhs=x[0][:, xcol:xcol + B].bitcast(FP8X4),
                rhs_scale=x[1][:, xcol:xcol + B],
                start=start,
                stop=stop,
            )

        def acc_pass(w, wcol, x, xcol):
            passes.append(wcol)
            mx_pass(acc, w, wcol, x, xcol, len(passes) == 1, len(passes) == N_PASS)

        def stage_mx2(s):
            if s < 0:
                return
            for h in range(2 if s < HM else 1):
                acc_pass(wq_tiles[(2, s)], h * P, xa_tiles[s], h * B)

        def stage_mx1(s, h):
            acc_pass(wq_tiles[(h, s)], 0, xb_tiles[(s, h)], 0)

        def stage_idle(s, n):
            if s < 0:
                return
            idle = dps.tile([P, B], F32, name="idle", tag="d")
            for r in range(n):
                mx_pass(idle, wq_tiles[(2, s)], 0, xa_tiles[s], 0, True, True)

        plan = {s: [] for s in range(NS)}
        for h, start, n in ((1, START_R, HM), (0, START_M, NS)):
            nxt = 0
            for s in range(start, NS):
                for r in range(2 if s % 2 == 0 else 1):
                    if nxt < n and nxt <= s:
                        plan[s].append((nxt, h))
                        nxt += 1

        K16 = HD // OCT
        ctx.enter_context(tc.manual_schedule())
        with tc.tile_pool(name="pro", bufs=1) as pro:
            F = pro.tile([P, NG, D], BF16, name="F")
            Fs = pro.tile([P, NG, D], BF16, name="Fs")
            nonzero = pro.tile([P, NG, D], BF16, name="nonzero")
            AI = pro.tile([P, NG, NM], F32, name="AI")
            FIn = pro.tile([P, NG, NM], BF16, name="FIn")
            Fraw = pro.tile([P, B // P, D], BF16, name="Fraw")
            one = pro.tile([P, 1], F32, name="one")

            def small(name):
                return pro.tile([P, NG], F32, name=name)

            Ssum, nz, sq, nqe, n2, nm, rn2 = [small(n) for n in ("Ssum", "nz", "sq", "nqe", "n2", "nm", "rn2")]
            SH = D - PACK + 1
            nc.gpsimd.memset(one[:], 1.0)
            nc.scalar.activation(out=one[:], in_=one[:], func=ACT.Sqrt)
            CUT = [0, 8, NG]
            queues = [nc.sync, nc.scalar, nc.sync, nc.scalar]
            for h in range(2):
                gs = slice(CUT[h], CUT[h + 1])
                for t in range(PACK):
                    queues[t].dma_start(out=F[t:P:PACK, gs, :], in_=feat_v[:, gs, :])
                for t in range(PACK):
                    queues[t].dma_start(out=Fs[t:P:PACK, gs, 0:SH], in_=feat_v[:, gs, t:t + SH])
                if h == 0:
                    nc.sync.dma_start(out=Fraw[:], in_=feat_n)
            nc.gpsimd.dma_start(out=bb[:], in_=b.partition_broadcast(P))
            load_w2(0)
            load_w2(1)
            for q in range(PACK):
                load_wn(Wb, HD, 0, q)
            load_w2(2)
            make_identity(nc, ident_bf[:])
            make_identity(nc, ident_f[:])
            nc.gpsimd.tensor_copy(out=mask_a[:], in_=ident_bf[:])
            nc.gpsimd.memset(mask_b[:], 0.0)
            FI = Fs[:, :, 0:SH:PACK]

            def head_count(h):
                gs = slice(CUT[h], CUT[h + 1])
                nc.vector.tensor_scalar(out=nonzero[:, gs, :], in0=F[:, gs, :], scalar1=0.0, scalar2=None, op0=ALU.not_equal)
                for w in (128, 64, 32, 16):
                    nc.vector.tensor_tensor(out=nonzero[:, gs, 0:w], in0=nonzero[:, gs, 0:w], in1=nonzero[:, gs, w:2 * w], op=ALU.add)
                nc.vector.tensor_reduce(out=nz[:, gs], in_=nonzero[:, gs, 0:16], axis=AX.X, op=ALU.add)

            def head_abs_i(h):
                gs = slice(CUT[h], CUT[h + 1])
                nc.vector.tensor_scalar(out=FIn[:, gs, :], in0=Fs[:, gs, 0:SH:PACK], scalar1=-1.0, scalar2=None, op0=ALU.mult)
                nc.vector.tensor_tensor(out=AI[:, gs, :], in0=Fs[:, gs, 0:SH:PACK], in1=FIn[:, gs, :], op=ALU.max)

            def head_scale(h):
                gs = slice(CUT[h], CUT[h + 1])
                nc.vector.tensor_tensor(out=sq[:, gs], in0=Ssum[:, gs], in1=Ssum[:, gs], op=ALU.mult)
                nc.vector.scalar_tensor_tensor(out=nqe[:, gs], in0=nz[:, gs], scalar=EPS_SQRT, in1=nz[:, gs], op0=ALU.mult, op1=ALU.mult)
                nc.vector.tensor_tensor(out=n2[:, gs], in0=sq[:, gs], in1=nqe[:, gs], op=ALU.add)
                nc.vector.tensor_scalar(out=nm[:, gs], in0=n2[:, gs], scalar1=EPS_NORM * EPS_NORM, scalar2=None, op0=ALU.max)
                nc.vector.reciprocal(out=rn2[:, gs], in_=nm[:, gs])
                nc.vector.tensor_scalar(out=beta[:, gs], in0=rn2[:, gs], scalar1=EPS_SQRT, scalar2=None, op0=ALU.mult)
                nc.vector.tensor_tensor(
                    out=alpha[:, gs, :], in0=AI[:, gs, :], in1=rn2[:, gs].unsqueeze(2).to_broadcast([P, CUT[h + 1] - CUT[h], NM]), op=ALU.mult
                )

            def head_abs(g0, g1):
                for g in range(g0, g1):
                    nc.scalar.activation(out=A[:, g, :], in_=F[:, g, :], func=ACT.Abs, accum_out=Ssum[:, g:g + 1])

            head_abs(0, 8)
            head_count(0)
            head_abs_i(0)
            head_scale(0)
            nc.scalar.activation(out=Fn[:], in_=Fraw[:], func=ACT.Sign)
            stage_tab_t(K16)
            nc.scalar.activation(out=SI[:], in_=FI[:, :, 0:HM], func=ACT.Sign)
            head_abs(8, 10)
            nc.gpsimd.tensor_scalar(out=Fm[:], in0=Fn[:, :, 0:HD], scalar1=1.0, scalar2=0.0, op0=ALU.mult, op1=ALU.add)
            stage_sqrt(0, 0)
            stage_sqrt(0, 1)
            stage_tab_s(K16)
            stage_tab_t(0)
            head_abs(10, 16)
            stage_tab_s(0)
            stage_sign(0, 0)
            head_count(1)
            stage_sign(0, 1)
            stage_t(0, 2)
            stage_t(0, 0)
            head_abs_i(1)
            head_scale(1)
            stage_e(0, 2)
            stage_sqrt(1, 0)
            stage_sqrt(0, 2)
            stage_sqrt(0, 3)
            stage_e(0, 0)
            stage_sqrt(1, 1)
            nc.scalar.activation(out=SIp[:], in_=FI[:, :, HM:NM].rearrange("q g m -> q m g").unsqueeze(3).to_broadcast([P, HM, NG, 2]), func=ACT.Sign)

        late[1] = ctx.enter_context(tc.tile_pool(name="xrpool", bufs=6))
        late[0] = ctx.enter_context(tc.tile_pool(name="xmpool", bufs=12))
        stage_sign(0, 2)
        stage_sign(0, 3)
        stage_t(0, 3)
        stage_t(0, 1)
        stage_w2t(0)
        stage_w2c(0)
        stage_w2t(1)
        stage_sqrt(1, 2)
        stage_sqrt(1, 3)
        for s in range(NS):
            old = plan.get(s - 1, [])
            old2 = plan.get(s - 2, [])
            if s % CH == 0:
                load_w2(s // CH + 3)
            for q in range(2 * PACK):
                if s == 3 * q // 4:
                    if q < PACK:
                        load_wn(Wb, HD, HD, q)
                    else:
                        load_wn(Wa, 0, 0, q - PACK)
            for w, h in old2:
                stage_mx1(w, h)
            stage_mx2(s - 1)
            if s > 0:
                stage_e(s, 2)
            stage_sign(s + 1, 0)
            for w, h in old:
                stage_wq(h, w)
            stage_w2c(s + 1)
            for w, h in plan[s]:
                if h == 0:
                    stage_w1c(w, h)
            stage_sqrt(s + 2, 0)
            stage_sqrt(s + 2, 1)
            if s % 2 == 0 and s // 2 + 1 < K16:
                stage_tab_t(s // 2 + 1)
            stage_tab_s(s // 2 + 1)
            stage_e(s, 3)
            stage_sign(s + 1, 1)
            stage_t(s + 1, 2)
            stage_idle(s - 1, 2)
            stage_wq(2, s)
            if s > 0:
                stage_e(s, 0)
            stage_sign(s + 1, 2)
            stage_w2t(s + 2)
            for w, h in plan[s]:
                if h == 1:
                    stage_w1c(w, h)
            stage_sqrt(s + 2, 2)
            stage_sqrt(s + 2, 3)
            stage_e(s, 1)
            stage_sign(s + 1, 3)
            stage_t(s + 1, 3)
            stage_sign2(s + 1)
            stage_mix(plan.get(s + 1, []))
            stage_idle(s - 1, 2)
            stage_t(s + 1, 0)
            if s == NS - 1:
                for w, h in plan[s]:
                    stage_wq(h, w)
            stage_q(s)
            stage_t(s + 1, 1)
            stage_q2(s, 1)
            stage_q2(s, 0)
        stage_mx2(NS - 1)
        for w, h in plan[NS - 2]:
            stage_mx1(w, h)
        for w, h in plan[NS - 1]:
            stage_mx1(w, h)

        accS = zpool.tile([P, B], F32, name="Z")
        res = zpool.tile([P, B // P, C], F32, name="Z")
        out_v = out.rearrange("(nb p) c -> p nb c", p=P)
        for nb in range(B // P):
            cs = slice(nb * P, (nb + 1) * P)
            nc.scalar.copy(out=accS[:, cs], in_=acc[:, cs])
            pso = tps.tile([P, P], F32, name="pso", tag="t")
            nc.tensor.transpose(out=pso[:], in_=accS[:, cs], identity=ident_f[:])
            nc.vector.tensor_tensor(out=res[:, nb, :], in0=pso[:], in1=bb[:], op=ALU.add)
            nc.sync.dma_start(out=out_v[:, nb, :], in_=res[:, nb, :])
